import numpy as np
import ml_dtypes


def mxq(x, axis, fmt="e4m3"):
    dtype, down = {"e4m3": (ml_dtypes.float8_e4m3fn, 7), "e5m2": (ml_dtypes.float8_e5m2, 14)}[fmt]
    v = np.moveaxis(np.asarray(x, np.float32).astype(ml_dtypes.bfloat16).astype(np.float64), axis, -1)
    blocks = v.reshape(v.shape[:-1] + (-1, 32))
    amax = np.abs(blocks).max(-1, keepdims=True)
    byte = np.maximum(np.where(amax > 0, np.frexp(amax)[1] - 1 + 127, 0) - down, 1)
    scale = np.exp2(byte - 127.0)
    codes = (blocks / scale).astype(np.float32).astype(dtype).astype(np.float64)
    return np.moveaxis((codes * scale).reshape(v.shape), -1, axis)


WIDE = False


def mx_kscale(k):
    if not WIDE:
        return np.ones(k)
    levels = np.array([10, -10, 5, -5, 0])
    a = np.random.permutation(np.resize(levels, k // 512 * 4)).reshape(k // 512, 4)
    idx = np.arange(k)
    return np.exp2(a[idx // 512, idx % 128 // 32])


BF16 = ml_dtypes.bfloat16


def bf(x):
    return np.asarray(x, np.float32).astype(BF16)


def f64(x):
    return np.asarray(x).astype(np.float64)


N, T, C, QK, VD, S, R = 1024, 3072, 256, 512, 512, 7, 8
SOFTMAX_SCALE = 1.0 / (0.01 * C ** 0.5)
EPS = 1e-12


def l2norm(x):
    n = np.sqrt(np.sum(x * x, axis=1, keepdims=True))
    return x / np.maximum(n, EPS)


def setup_inputs():
    ks = mx_kscale(QK)
    c = np.exp2(np.round(np.log2(np.sqrt(np.mean(ks * ks)))))
    p = np.random.standard_normal((R, QK)) / np.sqrt(R)
    q_dir = (np.random.standard_normal((N, R))[:, :, None] * p).sum(axis=1) + 0.5 * np.random.standard_normal((N, QK))
    k_dir = (np.random.standard_normal((T, R))[:, :, None] * p).sum(axis=1) + 0.5 * np.random.standard_normal((T, QK))
    gain = np.exp(0.5 * np.random.standard_normal((N, 1)))
    return {"q_emb": bf(q_dir * gain * ks), "keys": bf(l2norm(k_dir) / ks * c), "values": bf(2.0 * np.random.standard_normal((T, VD)))}


def reference(q_emb, keys, values):
    queries = l2norm(f64(q_emb))
    s = (mxq(queries, 1, "e4m3") @ mxq(f64(keys), 1, "e4m3").T) * SOFTMAX_SCALE
    e = np.exp(s - s.max(axis=1, keepdims=True))
    return (mxq(e, 1, "e4m3") @ mxq(f64(values), 0, "e4m3")) / e.sum(axis=1, keepdims=True)

@@ -1,0 +1,237 @@
+from contextlib import ExitStack
+
+import concourse.mybir as mybir
+from concourse.masks import make_identity
+
+F32 = mybir.dt.float32
+BF16 = mybir.dt.bfloat16
+U32 = mybir.dt.uint32
+U8 = mybir.dt.uint8
+FP8X4 = mybir.dt.float8_e4m3fn_x4
+ALU = mybir.AluOpType
+ACT = mybir.ActivationFunctionType
+AX = mybir.AxisListType
+
+P = 128
+N, T, QK, VD = 1024, 3072, 512, 512
+NT = N // P
+TC = T // 512
+SCALE = 6.25
+EPS = 1e-12
+FLOPS = 2 * N * T * QK + 2 * N * T * VD
+
+GPSIMD_TILES = 0
+SS_COL = {0: 0, 1: 1, 4: 2, 5: 3, 2: 4, 3: 5, 6: 6, 7: 7}
+
+
+def tile_contextrcnn_pb_kernel(tc, q_emb, keys, values, out):
+    nc = tc.nc
+    with ExitStack() as ctx:
+        keep = ctx.enter_context(tc.tile_pool(name="keep", bufs=1))
+        work = ctx.enter_context(tc.tile_pool(name="work", bufs=2))
+        psum = ctx.enter_context(tc.psum_pool(name="psum", bufs=1))
+
+        q_raw = keep.tile([P, NT, QK], BF16, name="q_raw")
+        q_view = q_emb.rearrange("(p i) k -> p i k", i=NT)
+        for h in range(2):
+            nc.sync.dma_start(out=q_raw[:, 4 * h : 4 * h + 4, :], in_=q_view[:, 4 * h : 4 * h + 4, :])
+        k_raw = []
+        for c in range(TC):
+            kr = keep.tile([P, 4, QK], BF16, name="k_raw%d" % c)
+            nc.sync.dma_start(out=kr[:], in_=keys[512 * c : 512 * c + 512, :].rearrange("(p a) k -> p a k", a=4))
+            k_raw.append(kr)
+        v_raw = []
+        for g in range(TC):
+            vr = keep.tile([P, 4, VD], BF16, name="v_raw%d" % g)
+            nc.sync.dma_start(out=vr[:], in_=values[512 * g : 512 * g + 512, :].rearrange("(p j) w -> p j w", j=4))
+            v_raw.append(vr)
+
+        ident_bf = keep.tile([P, P], BF16, name="ident_bf")
+        make_identity(nc, ident_bf[:])
+        ident_f = keep.tile([P, P], F32, name="ident_f")
+        make_identity(nc, ident_f[:])
+        one = keep.tile([P, 1], F32, name="one")
+        nc.vector.memset(one[:], 1.0)
+        warm = keep.tile([P, 2], F32, name="warm")
+        nc.scalar.activation(out=warm[:, 0:1], in_=one[:], func=ACT.Sqrt)
+
+        ss_s = keep.tile([P, 4], F32, name="ss_s")
+        ss_v = keep.tile([P, 4], F32, name="ss_v")
+        nrm = keep.tile([P, NT], F32, name="nrm")
+        nrm_c = keep.tile([P, NT], F32, name="nrm_c")
+        rn = keep.tile([P, NT], F32, name="rn")
+        for i in (0, 1, 4, 5):
+            sq = work.tile([P, QK], BF16, tag="sq", name="sq")
+            nc.scalar.activation(out=sq[:], in_=q_raw[:, i, :], func=ACT.Square, accum_out=ss_s[:, SS_COL[i] : SS_COL[i] + 1])
+        for i in (2, 3, 6, 7):
+            sqf = work.tile([P, QK], F32, tag="sqf", name="sqf")
+            nc.vector.scalar_tensor_tensor(out=sqf[:], in0=q_raw[:, i, :], scalar=1.0, in1=q_raw[:, i, :], op0=ALU.mult, op1=ALU.mult,
+                                           accum_out=ss_v[:, SS_COL[i] - 4 : SS_COL[i] - 3])
+        nc.scalar.activation(out=nrm[:, 0:4], in_=ss_s[:], func=ACT.Sqrt)
+        nc.scalar.activation(out=nrm[:, 4:8], in_=ss_v[:], func=ACT.Sqrt)
+        nc.scalar.activation(out=warm[:, 1:2], in_=one[:], func=ACT.Exp)
+        nc.vector.tensor_scalar_max(out=nrm_c[:], in0=nrm[:], scalar1=EPS)
+        nc.vector.reciprocal(out=rn[:], in_=nrm_c[:])
+
+        q_words = keep.tile([P, NT * P], U32, name="q_words", align_bytes=64)
+        q_scales = keep.tile([P, NT * P], U8, name="q_scales", align_bytes=64)
+
+        def query_pair(b):
+            qn = work.tile([P, 2, QK], BF16, tag="qn", name="qn")
+            for ii in range(2):
+                i = 2 * b + ii
+                nc.vector.tensor_scalar(out=qn[:, ii, :], in0=q_raw[:, i, :], scalar1=rn[:, SS_COL[i] : SS_COL[i] + 1], scalar2=None, op0=ALU.mult)
+            qt = psum.tile([P, 2, 4, P], BF16, tag="t", bufs=3, name="qt")
+            for ii in range(2):
+                src = qn[:, ii, :].rearrange("p (u m e) -> p u e m", u=2, e=2)
+                for u in range(2):
+                    for e in range(2):
+                        nc.tensor.transpose(qt[:, ii, 2 * u + e, :], src[:, u, e, :], ident_bf[:])
+            q_grp = work.tile([P, 1024], BF16, tag="q_grp", align_bytes=64, name="q_grp")
+            nc.scalar.copy(out=q_grp[:].rearrange("p (i n t) -> p i n t", i=2, t=4), in_=qt[:].rearrange("p i t n -> p i n t"))
+            nc.vector.quantize_mx(
+                out=q_words[:, 256 * b : 256 * b + 256].bitcast(FP8X4),
+                scales=q_scales[:, 256 * b : 256 * b + 256],
+                in_=q_grp[:],
+            )
+
+        k_words = keep.tile([P, T], U32, name="k_words", align_bytes=64)
+        k_scales = keep.tile([P, T], U8, name="k_scales", align_bytes=64)
+
+        def key_chunk(c):
+            kw = k_raw[c][:].rearrange("p a k -> p (a k)").bitcast(F32)
+            k_grp = work.tile([P, 2048], BF16, tag="k_grp", align_bytes=64, name="k_grp")
+            gw = k_grp[:].bitcast(F32).rearrange("p (a t u) -> p a t u", a=4, u=2)
+            for h in range(2):
+                kt = psum.tile([P, 2, 2, P], F32, tag="t", bufs=3, name="kt")
+                for a2 in range(2):
+                    for u in range(2):
+                        col = 256 * (2 * h + a2) + 128 * u
+                        nc.tensor.transpose(kt[:, a2, u, :], kw[:, col : col + 128], ident_f[:])
+                nc.scalar.copy(out=gw[:, 2 * h : 2 * h + 2, :, :], in_=kt[:].rearrange("p a u t -> p a t u"))
+            nc.vector.quantize_mx(
+                out=k_words[:, 512 * c : 512 * c + 512].bitcast(FP8X4),
+                scales=k_scales[:, 512 * c : 512 * c + 512],
+                in_=k_grp[:],
+            )
+
+        v_words = keep.tile([P, TC * VD], U32, name="v_words", align_bytes=64)
+        v_scales = keep.tile([P, TC * VD], U8, name="v_scales", align_bytes=64)
+
+        def value_chunk(g):
+            v_grp = work.tile([P, VD, 4], BF16, tag="v_grp", bufs=3, align_bytes=64, name="v_grp")
+            nc.vector.tensor_copy(
+                out=v_grp[:].rearrange("p (c i) t -> p c t i", i=4),
+                in_=v_raw[g][:].rearrange("p t (c i) -> p c t i", i=4),
+            )
+            nc.vector.quantize_mx(
+                out=v_words[:, VD * g : VD * g + VD].bitcast(FP8X4),
+                scales=v_scales[:, VD * g : VD * g + VD],
+                in_=v_grp[:].rearrange("p w t -> p (w t)"),
+            )
+
+        s_sb, mins, nbias, e_wd, e_sc, rinv = {}, {}, {}, {}, {}, {}
+
+        def scores(i, c):
+            if c == 0:
+                s_sb[i] = work.tile([P, T], F32, tag="s_sb", bufs=3, name="s_sb")
+                mins[i] = work.tile([P, TC], F32, tag="mins", bufs=4, name="mins")
+            s_ps = psum.tile([P, 512], F32, tag="s", bufs=3, name="s_ps")
+            nc.tensor.matmul_mx(
+                out=s_ps[:],
+                lhsT=q_words[:, P * i : P * i + P].bitcast(FP8X4),
+                lhsT_scale=q_scales[:, P * i : P * i + P],
+                rhs=k_words[:, 512 * c : 512 * c + 512].bitcast(FP8X4),
+                rhs_scale=k_scales[:, 512 * c : 512 * c + 512],
+                start=True,
+                stop=True,
+            )
+            nc.vector.tensor_scalar(
+                out=s_sb[i][:, 512 * c : 512 * c + 512], in0=s_ps[:], scalar1=-SCALE, scalar2=None,
+                op0=ALU.mult, op1=ALU.min, accum_out=mins[i][:, c : c + 1],
+            )
+            if c == TC - 1:
+                nbias[i] = work.tile([P, 1], F32, tag="nbias", bufs=4, name="nbias")
+                nc.vector.tensor_reduce(out=nbias[i][:], in_=mins[i][:], axis=AX.X, op=ALU.min)
+
+        def softmax(i):
+            pieces = 1 if i < NT - 1 else 3
+            width = T // pieces
+            e_sb = work.tile([P, T], BF16, tag="e_sb", bufs=2, name="e_sb")
+            rsum = work.tile([P, pieces], F32, tag="rsum", bufs=3, name="rsum")
+            for h in range(pieces):
+                cols = slice(width * h, width * h + width)
+                nc.scalar.activation(out=e_sb[:, cols], in_=s_sb[i][:, cols], func=ACT.Exp, bias=nbias[i][:], scale=-1.0,
+                                     accum_out=rsum[:, h : h + 1])
+            e_grp = work.tile([P, T], BF16, tag="e_grp", bufs=2, align_bytes=64, name="e_grp")
+            e_wd[i] = work.tile([P, T // 4], U32, tag="e_wd", bufs=4, align_bytes=64, name="e_wd")
+            e_sc[i] = work.tile([P, T // 4], U8, tag="e_sc", bufs=4, align_bytes=64, name="e_sc")
+            via_gpsimd = i < GPSIMD_TILES
+            if via_gpsimd:
+                e_t = work.tile([P, T], BF16, tag="e_t", bufs=2, name="e_t")
+            for h in range(3):
+                et = psum.tile([P, 2, 4, P], BF16, tag="t", bufs=3, name="et")
+                for gg in range(2):
+                    for j in range(4):
+                        col = 1024 * h + 512 * gg + 128 * j
+                        nc.tensor.transpose(et[:, gg, j, :], e_sb[:, col : col + 128], ident_bf[:])
+                cols = slice(1024 * h, 1024 * h + 1024)
+                dst = e_grp[:, cols].rearrange("p (g n j) -> p g n j", g=2, j=4)
+                if via_gpsimd:
+                    nc.scalar.copy(out=e_t[:, cols], in_=et[:].rearrange("p g j n -> p (g j n)"))
+                    nc.gpsimd.tensor_scalar(out=dst, in0=e_t[:, cols].rearrange("p (g j n) -> p g n j", g=2, j=4),
+                                            scalar1=1.0, scalar2=0.0, op0=ALU.mult, op1=ALU.add)
+                else:
+                    on_vector = (i >= NT - 2 and h == 1) or (i == NT - 2 and h == 2)
+                    eng_copy = nc.vector.tensor_copy if on_vector else nc.scalar.copy
+                    eng_copy(out=dst, in_=et[:].rearrange("p g j n -> p g n j"))
+            for h in range(3):
+                nc.vector.quantize_mx(
+                    out=e_wd[i][:, 256 * h : 256 * h + 256].bitcast(FP8X4),
+                    scales=e_sc[i][:, 256 * h : 256 * h + 256],
+                    in_=e_grp[:, 1024 * h : 1024 * h + 1024],
+                )
+            rinv[i] = work.tile([P, 1], F32, tag="rinv", bufs=4, name="rinv")
+            if pieces == 1:
+                nc.vector.reciprocal(out=rinv[i][:], in_=rsum[:])
+            else:
+                tot = work.tile([P, 1], F32, tag="tot", name="tot")
+                nc.vector.tensor_reduce(out=tot[:], in_=rsum[:], axis=AX.X, op=ALU.add)
+                nc.vector.reciprocal(out=rinv[i][:], in_=tot[:])
+
+        out_view = out.rearrange("(p i) d -> p i d", i=NT)
+
+        def weighted_sum(i):
+            o_ps = psum.tile([P, VD], F32, tag="o", bufs=2, name="o_ps")
+            for g in range(TC):
+                nc.tensor.matmul_mx(
+                    out=o_ps[:],
+                    lhsT=e_wd[i][:, P * g : P * g + P].bitcast(FP8X4),
+                    lhsT_scale=e_sc[i][:, P * g : P * g + P],
+                    rhs=v_words[:, VD * g : VD * g + VD].bitcast(FP8X4),
+                    rhs_scale=v_scales[:, VD * g : VD * g + VD],
+                    start=(g == 0),
+                    stop=(g == TC - 1),
+                )
+            o_sb = work.tile([P, VD], F32, tag="o_sb", bufs=3, name="o_sb")
+            nc.vector.tensor_scalar(out=o_sb[:], in0=o_ps[:], scalar1=rinv[i][:], scalar2=None, op0=ALU.mult)
+            nc.sync.dma_start(out=out_view[:, i, :], in_=o_sb[:])
+
+        query_pair(0)
+        query_pair(1)
+        for c in range(TC):
+            key_chunk(c)
+            scores(0, c)
+        for c in range(TC):
+            scores(1, c)
+        for g in range(TC):
+            value_chunk(g)
+        for i in range(NT):
+            softmax(i)
+            if i + 2 < NT:
+                for c in range(TC):
+                    scores(i + 2, c)
+            if i == 0:
+                query_pair(2)
+                query_pair(3)
+            weighted_sum(i)

@@ -20,7 +20,7 @@ SCALE = 6.25
 EPS = 1e-12
 FLOPS = 2 * N * T * QK + 2 * N * T * VD
 
-GPSIMD_TILES = 0
+GPSIMD_TILES = 6
 SS_COL = {0: 0, 1: 1, 4: 2, 5: 3, 2: 4, 3: 5, 6: 6, 7: 7}
 
 
@@ -120,10 +120,10 @@ def tile_contextrcnn_pb_kernel(tc, q_emb, keys, values, out):
 
         def value_chunk(g):
             v_grp = work.tile([P, VD, 4], BF16, tag="v_grp", bufs=3, align_bytes=64, name="v_grp")
-            nc.vector.tensor_copy(
-                out=v_grp[:].rearrange("p (c i) t -> p c t i", i=4),
-                in_=v_raw[g][:].rearrange("p t (c i) -> p c t i", i=4),
-            )
+            for half in range(2):
+                w = slice(256 * half, 256 * half + 256)
+                nc.gpsimd.tensor_scalar(out=v_grp[:, w, :], in0=v_raw[g][:, :, w].rearrange("p t w -> p w t"),
+                                        scalar1=1.0, scalar2=0.0, op0=ALU.mult, op1=ALU.add)
             nc.vector.quantize_mx(
                 out=v_words[:, VD * g : VD * g + VD].bitcast(FP8X4),
                 scales=v_scales[:, VD * g : VD * g + VD],
@@ -182,7 +182,7 @@ def tile_contextrcnn_pb_kernel(tc, q_emb, keys, values, out):
                     nc.gpsimd.tensor_scalar(out=dst, in0=e_t[:, cols].rearrange("p (g j n) -> p g n j", g=2, j=4),
                                             scalar1=1.0, scalar2=0.0, op0=ALU.mult, op1=ALU.add)
                 else:
-                    on_vector = (i >= NT - 2 and h == 1) or (i == NT - 2 and h == 2)
+                    on_vector = (i == NT - 2) or h == 1
                     eng_copy = nc.vector.tensor_copy if on_vector else nc.scalar.copy
                     eng_copy(out=dst, in_=et[:].rearrange("p g j n -> p g n j"))
             for h in range(3):

@@ -20,16 +20,23 @@ SCALE = 6.25
 EPS = 1e-12
 FLOPS = 2 * N * T * QK + 2 * N * T * VD
 
-GPSIMD_TILES = 6
+GPSIMD_TILES = 5
 SS_COL = {0: 0, 1: 1, 4: 2, 5: 3, 2: 4, 3: 5, 6: 6, 7: 7}
 
 
 def tile_contextrcnn_pb_kernel(tc, q_emb, keys, values, out):
     nc = tc.nc
     with ExitStack() as ctx:
+        ctx.enter_context(tc.manual_schedule())
         keep = ctx.enter_context(tc.tile_pool(name="keep", bufs=1))
         work = ctx.enter_context(tc.tile_pool(name="work", bufs=2))
         psum = ctx.enter_context(tc.psum_pool(name="psum", bufs=1))
+
+        def copy_on(engine, out_ap, in_ap):
+            if engine == "V":
+                nc.vector.tensor_copy(out=out_ap, in_=in_ap)
+            else:
+                nc.scalar.copy(out=out_ap, in_=in_ap)
 
         q_raw = keep.tile([P, NT, QK], BF16, name="q_raw")
         q_view = q_emb.rearrange("(p i) k -> p i k", i=NT)
@@ -60,85 +67,95 @@ def tile_contextrcnn_pb_kernel(tc, q_emb, keys, values, out):
         nrm = keep.tile([P, NT], F32, name="nrm")
         nrm_c = keep.tile([P, NT], F32, name="nrm_c")
         rn = keep.tile([P, NT], F32, name="rn")
-        for i in (0, 1, 4, 5):
-            sq = work.tile([P, QK], BF16, tag="sq", name="sq")
-            nc.scalar.activation(out=sq[:], in_=q_raw[:, i, :], func=ACT.Square, accum_out=ss_s[:, SS_COL[i] : SS_COL[i] + 1])
-        for i in (2, 3, 6, 7):
-            sqf = work.tile([P, QK], F32, tag="sqf", name="sqf")
-            nc.vector.scalar_tensor_tensor(out=sqf[:], in0=q_raw[:, i, :], scalar=1.0, in1=q_raw[:, i, :], op0=ALU.mult, op1=ALU.mult,
-                                           accum_out=ss_v[:, SS_COL[i] - 4 : SS_COL[i] - 3])
-        nc.scalar.activation(out=nrm[:, 0:4], in_=ss_s[:], func=ACT.Sqrt)
-        nc.scalar.activation(out=nrm[:, 4:8], in_=ss_v[:], func=ACT.Sqrt)
-        nc.scalar.activation(out=warm[:, 1:2], in_=one[:], func=ACT.Exp)
-        nc.vector.tensor_scalar_max(out=nrm_c[:], in0=nrm[:], scalar1=EPS)
-        nc.vector.reciprocal(out=rn[:], in_=nrm_c[:])
-
+        qn = keep.tile([P, NT, QK], BF16, name="qn")
         q_words = keep.tile([P, NT * P], U32, name="q_words", align_bytes=64)
         q_scales = keep.tile([P, NT * P], U8, name="q_scales", align_bytes=64)
+        q_ps, q_grp = {}, {}
 
-        def query_pair(b):
-            qn = work.tile([P, 2, QK], BF16, tag="qn", name="qn")
+        def norms():
+            for i in (0, 1, 4, 5):
+                sq = work.tile([P, QK], BF16, tag="sq", name="sq")
+                nc.scalar.activation(out=sq[:], in_=q_raw[:, i, :], func=ACT.Square, accum_out=ss_s[:, SS_COL[i] : SS_COL[i] + 1])
+            for i in (2, 3, 6, 7):
+                sqf = work.tile([P, QK], F32, tag="sqf", name="sqf")
+                nc.vector.scalar_tensor_tensor(out=sqf[:], in0=q_raw[:, i, :], scalar=1.0, in1=q_raw[:, i, :], op0=ALU.mult, op1=ALU.mult,
+                                               accum_out=ss_v[:, SS_COL[i] - 4 : SS_COL[i] - 3])
+            nc.scalar.activation(out=nrm[:, 0:4], in_=ss_s[:], func=ACT.Sqrt)
+            nc.scalar.activation(out=nrm[:, 4:8], in_=ss_v[:], func=ACT.Sqrt)
+            nc.scalar.activation(out=warm[:, 1:2], in_=one[:], func=ACT.Exp)
+            nc.vector.tensor_scalar_max(out=nrm_c[:], in0=nrm[:], scalar1=EPS)
+            nc.vector.reciprocal(out=rn[:], in_=nrm_c[:])
+            for i in range(NT):
+                nc.vector.tensor_scalar(out=qn[:, i, :], in0=q_raw[:, i, :], scalar1=rn[:, SS_COL[i] : SS_COL[i] + 1], scalar2=None, op0=ALU.mult)
+
+        def q_transpose(b):
+            q_ps[b] = psum.tile([P, 2, 4, P], BF16, tag="t", bufs=3, name="qt")
             for ii in range(2):
-                i = 2 * b + ii
-                nc.vector.tensor_scalar(out=qn[:, ii, :], in0=q_raw[:, i, :], scalar1=rn[:, SS_COL[i] : SS_COL[i] + 1], scalar2=None, op0=ALU.mult)
-            qt = psum.tile([P, 2, 4, P], BF16, tag="t", bufs=3, name="qt")
-            for ii in range(2):
-                src = qn[:, ii, :].rearrange("p (u m e) -> p u e m", u=2, e=2)
+                src = qn[:, 2 * b + ii, :].rearrange("p (u m e) -> p u e m", u=2, e=2)
                 for u in range(2):
                     for e in range(2):
-                        nc.tensor.transpose(qt[:, ii, 2 * u + e, :], src[:, u, e, :], ident_bf[:])
-            q_grp = work.tile([P, 1024], BF16, tag="q_grp", align_bytes=64, name="q_grp")
-            nc.scalar.copy(out=q_grp[:].rearrange("p (i n t) -> p i n t", i=2, t=4), in_=qt[:].rearrange("p i t n -> p i n t"))
+                        nc.tensor.transpose(q_ps[b][:, ii, 2 * u + e, :], src[:, u, e, :], ident_bf[:])
+
+        def q_exit(b, engine):
+            q_grp[b] = work.tile([P, 1024], BF16, tag="q_grp", align_bytes=64, name="q_grp")
+            copy_on(engine, q_grp[b][:].rearrange("p (i n t) -> p i n t", i=2, t=4), q_ps[b][:].rearrange("p i t n -> p i n t"))
+
+        def q_quantise(b):
             nc.vector.quantize_mx(
                 out=q_words[:, 256 * b : 256 * b + 256].bitcast(FP8X4),
                 scales=q_scales[:, 256 * b : 256 * b + 256],
-                in_=q_grp[:],
+                in_=q_grp[b][:],
             )
 
         k_words = keep.tile([P, T], U32, name="k_words", align_bytes=64)
         k_scales = keep.tile([P, T], U8, name="k_scales", align_bytes=64)
+        k_ps, k_grp = {}, {}
 
-        def key_chunk(c):
+        def k_transpose(c, h):
             kw = k_raw[c][:].rearrange("p a k -> p (a k)").bitcast(F32)
-            k_grp = work.tile([P, 2048], BF16, tag="k_grp", align_bytes=64, name="k_grp")
-            gw = k_grp[:].bitcast(F32).rearrange("p (a t u) -> p a t u", a=4, u=2)
-            for h in range(2):
-                kt = psum.tile([P, 2, 2, P], F32, tag="t", bufs=3, name="kt")
-                for a2 in range(2):
-                    for u in range(2):
-                        col = 256 * (2 * h + a2) + 128 * u
-                        nc.tensor.transpose(kt[:, a2, u, :], kw[:, col : col + 128], ident_f[:])
-                nc.scalar.copy(out=gw[:, 2 * h : 2 * h + 2, :, :], in_=kt[:].rearrange("p a u t -> p a t u"))
+            k_ps[c, h] = psum.tile([P, 2, 2, P], F32, tag="t", bufs=3, name="kt")
+            for a2 in range(2):
+                for u in range(2):
+                    col = 256 * (2 * h + a2) + 128 * u
+                    nc.tensor.transpose(k_ps[c, h][:, a2, u, :], kw[:, col : col + 128], ident_f[:])
+
+        def k_exit(c, h, engine):
+            if h == 0:
+                k_grp[c] = work.tile([P, 2048], BF16, tag="k_grp", align_bytes=64, name="k_grp")
+            gw = k_grp[c][:].bitcast(F32).rearrange("p (a t u) -> p a t u", a=4, u=2)
+            copy_on(engine, gw[:, 2 * h : 2 * h + 2, :, :], k_ps[c, h][:].rearrange("p a u t -> p a t u"))
+
+        def k_quantise(c):
             nc.vector.quantize_mx(
                 out=k_words[:, 512 * c : 512 * c + 512].bitcast(FP8X4),
                 scales=k_scales[:, 512 * c : 512 * c + 512],
-                in_=k_grp[:],
+                in_=k_grp[c][:],
             )
 
         v_words = keep.tile([P, TC * VD], U32, name="v_words", align_bytes=64)
         v_scales = keep.tile([P, TC * VD], U8, name="v_scales", align_bytes=64)
+        v_grp = {}
 
-        def value_chunk(g):
-            v_grp = work.tile([P, VD, 4], BF16, tag="v_grp", bufs=3, align_bytes=64, name="v_grp")
+        def v_regroup(g):
+            v_grp[g] = work.tile([P, VD, 4], BF16, tag="v_grp", bufs=TC, align_bytes=64, name="v_grp")
             for half in range(2):
                 w = slice(256 * half, 256 * half + 256)
-                nc.gpsimd.tensor_scalar(out=v_grp[:, w, :], in0=v_raw[g][:, :, w].rearrange("p t w -> p w t"),
+                nc.gpsimd.tensor_scalar(out=v_grp[g][:, w, :], in0=v_raw[g][:, :, w].rearrange("p t w -> p w t"),
                                         scalar1=1.0, scalar2=0.0, op0=ALU.mult, op1=ALU.add)
+
+        def v_quantise(g):
             nc.vector.quantize_mx(
                 out=v_words[:, VD * g : VD * g + VD].bitcast(FP8X4),
                 scales=v_scales[:, VD * g : VD * g + VD],
-                in_=v_grp[:].rearrange("p w t -> p (w t)"),
+                in_=v_grp[g][:].rearrange("p w t -> p (w t)"),
             )
 
-        s_sb, mins, nbias, e_wd, e_sc, rinv = {}, {}, {}, {}, {}, {}
+        s_ps, s_sb, mins, nbias, e_sb, rsum, e_ps, e_t, e_grp, e_wd, e_sc, rinv, o_ps = {}, {}, {}, {}, {}, {}, {}, {}, {}, {}, {}, {}, {}
 
-        def scores(i, c):
-            if c == 0:
-                s_sb[i] = work.tile([P, T], F32, tag="s_sb", bufs=3, name="s_sb")
-                mins[i] = work.tile([P, TC], F32, tag="mins", bufs=4, name="mins")
-            s_ps = psum.tile([P, 512], F32, tag="s", bufs=3, name="s_ps")
+        def score_pass(i, c):
+            s_ps[i, c] = psum.tile([P, 512], F32, tag="s", bufs=3, name="s_ps")
             nc.tensor.matmul_mx(
-                out=s_ps[:],
+                out=s_ps[i, c][:],
                 lhsT=q_words[:, P * i : P * i + P].bitcast(FP8X4),
                 lhsT_scale=q_scales[:, P * i : P * i + P],
                 rhs=k_words[:, 512 * c : 512 * c + 512].bitcast(FP8X4),
@@ -146,92 +163,190 @@ def tile_contextrcnn_pb_kernel(tc, q_emb, keys, values, out):
                 start=True,
                 stop=True,
             )
+
+        def score_exit(i, c):
+            if c == 0:
+                s_sb[i] = work.tile([P, T], F32, tag="s_sb", bufs=2, name="s_sb")
+                mins[i] = work.tile([P, TC], F32, tag="mins", bufs=3, name="mins")
             nc.vector.tensor_scalar(
-                out=s_sb[i][:, 512 * c : 512 * c + 512], in0=s_ps[:], scalar1=-SCALE, scalar2=None,
+                out=s_sb[i][:, 512 * c : 512 * c + 512], in0=s_ps[i, c][:], scalar1=-SCALE, scalar2=None,
                 op0=ALU.mult, op1=ALU.min, accum_out=mins[i][:, c : c + 1],
             )
-            if c == TC - 1:
-                nbias[i] = work.tile([P, 1], F32, tag="nbias", bufs=4, name="nbias")
-                nc.vector.tensor_reduce(out=nbias[i][:], in_=mins[i][:], axis=AX.X, op=ALU.min)
 
-        def softmax(i):
-            pieces = 1 if i < NT - 1 else 3
+        def bias(i):
+            nbias[i] = work.tile([P, 1], F32, tag="nbias", bufs=3, name="nbias")
+            nc.vector.tensor_reduce(out=nbias[i][:], in_=mins[i][:], axis=AX.X, op=ALU.min)
+
+        def exponential(i, piece, pieces):
+            if piece == 0:
+                e_sb[i] = work.tile([P, T], BF16, tag="e_sb", bufs=2, name="e_sb")
+                rsum[i] = work.tile([P, pieces], F32, tag="rsum", bufs=5, name="rsum")
             width = T // pieces
-            e_sb = work.tile([P, T], BF16, tag="e_sb", bufs=2, name="e_sb")
-            rsum = work.tile([P, pieces], F32, tag="rsum", bufs=3, name="rsum")
-            for h in range(pieces):
-                cols = slice(width * h, width * h + width)
-                nc.scalar.activation(out=e_sb[:, cols], in_=s_sb[i][:, cols], func=ACT.Exp, bias=nbias[i][:], scale=-1.0,
-                                     accum_out=rsum[:, h : h + 1])
-            e_grp = work.tile([P, T], BF16, tag="e_grp", bufs=2, align_bytes=64, name="e_grp")
-            e_wd[i] = work.tile([P, T // 4], U32, tag="e_wd", bufs=4, align_bytes=64, name="e_wd")
-            e_sc[i] = work.tile([P, T // 4], U8, tag="e_sc", bufs=4, align_bytes=64, name="e_sc")
-            via_gpsimd = i < GPSIMD_TILES
-            if via_gpsimd:
-                e_t = work.tile([P, T], BF16, tag="e_t", bufs=2, name="e_t")
-            for h in range(3):
-                et = psum.tile([P, 2, 4, P], BF16, tag="t", bufs=3, name="et")
-                for gg in range(2):
-                    for j in range(4):
-                        col = 1024 * h + 512 * gg + 128 * j
-                        nc.tensor.transpose(et[:, gg, j, :], e_sb[:, col : col + 128], ident_bf[:])
-                cols = slice(1024 * h, 1024 * h + 1024)
-                dst = e_grp[:, cols].rearrange("p (g n j) -> p g n j", g=2, j=4)
-                if via_gpsimd:
-                    nc.scalar.copy(out=e_t[:, cols], in_=et[:].rearrange("p g j n -> p (g j n)"))
-                    nc.gpsimd.tensor_scalar(out=dst, in0=e_t[:, cols].rearrange("p (g j n) -> p g n j", g=2, j=4),
-                                            scalar1=1.0, scalar2=0.0, op0=ALU.mult, op1=ALU.add)
-                else:
-                    on_vector = (i == NT - 2) or h == 1
-                    eng_copy = nc.vector.tensor_copy if on_vector else nc.scalar.copy
-                    eng_copy(out=dst, in_=et[:].rearrange("p g j n -> p g n j"))
-            for h in range(3):
-                nc.vector.quantize_mx(
-                    out=e_wd[i][:, 256 * h : 256 * h + 256].bitcast(FP8X4),
-                    scales=e_sc[i][:, 256 * h : 256 * h + 256],
-                    in_=e_grp[:, 1024 * h : 1024 * h + 1024],
-                )
+            cols = slice(width * piece, width * piece + width)
+            nc.scalar.activation(out=e_sb[i][:, cols], in_=s_sb[i][:, cols], func=ACT.Exp, bias=nbias[i][:], scale=-1.0,
+                                 accum_out=rsum[i][:, piece : piece + 1])
+
+        def e_transpose(i, h):
+            e_ps[i, h] = psum.tile([P, 2, 4, P], BF16, tag="t", bufs=3, name="et")
+            for gg in range(2):
+                for j in range(4):
+                    col = 1024 * h + 512 * gg + 128 * j
+                    nc.tensor.transpose(e_ps[i, h][:, gg, j, :], e_sb[i][:, col : col + 128], ident_bf[:])
+
+        def e_exit(i, h, engine):
+            if i not in e_grp:
+                e_grp[i] = work.tile([P, T], BF16, tag="e_grp", bufs=2, align_bytes=64, name="e_grp")
+            cols = slice(1024 * h, 1024 * h + 1024)
+            dst = e_grp[i][:, cols].rearrange("p (g n j) -> p g n j", g=2, j=4)
+            if i < GPSIMD_TILES:
+                if i not in e_t:
+                    e_t[i] = work.tile([P, T], BF16, tag="e_t", bufs=2, name="e_t")
+                copy_on(engine, e_t[i][:, cols], e_ps[i, h][:].rearrange("p g j n -> p (g j n)"))
+                nc.gpsimd.tensor_scalar(out=dst, in0=e_t[i][:, cols].rearrange("p (g j n) -> p g n j", g=2, j=4),
+                                        scalar1=1.0, scalar2=0.0, op0=ALU.mult, op1=ALU.add)
+            else:
+                copy_on(engine, dst, e_ps[i, h][:].rearrange("p g j n -> p g n j"))
+
+        def e_quantise(i, h):
+            if h == 0:
+                e_wd[i] = work.tile([P, T // 4], U32, tag="e_wd", bufs=3, align_bytes=64, name="e_wd")
+                e_sc[i] = work.tile([P, T // 4], U8, tag="e_sc", bufs=3, align_bytes=64, name="e_sc")
+            nc.vector.quantize_mx(
+                out=e_wd[i][:, 256 * h : 256 * h + 256].bitcast(FP8X4),
+                scales=e_sc[i][:, 256 * h : 256 * h + 256],
+                in_=e_grp[i][:, 1024 * h : 1024 * h + 1024],
+            )
+
+        def row_scale(i, pieces):
             rinv[i] = work.tile([P, 1], F32, tag="rinv", bufs=4, name="rinv")
             if pieces == 1:
-                nc.vector.reciprocal(out=rinv[i][:], in_=rsum[:])
+                nc.vector.reciprocal(out=rinv[i][:], in_=rsum[i][:])
             else:
                 tot = work.tile([P, 1], F32, tag="tot", name="tot")
-                nc.vector.tensor_reduce(out=tot[:], in_=rsum[:], axis=AX.X, op=ALU.add)
+                nc.vector.tensor_reduce(out=tot[:], in_=rsum[i][:], axis=AX.X, op=ALU.add)
                 nc.vector.reciprocal(out=rinv[i][:], in_=tot[:])
+
+        def value_pass(i, g):
+            if g == 0:
+                o_ps[i] = psum.tile([P, VD], F32, tag="o", bufs=2, name="o_ps")
+            nc.tensor.matmul_mx(
+                out=o_ps[i][:],
+                lhsT=e_wd[i][:, P * g : P * g + P].bitcast(FP8X4),
+                lhsT_scale=e_sc[i][:, P * g : P * g + P],
+                rhs=v_words[:, VD * g : VD * g + VD].bitcast(FP8X4),
+                rhs_scale=v_scales[:, VD * g : VD * g + VD],
+                start=(g == 0),
+                stop=(g == TC - 1),
+            )
 
         out_view = out.rearrange("(p i) d -> p i d", i=NT)
 
-        def weighted_sum(i):
-            o_ps = psum.tile([P, VD], F32, tag="o", bufs=2, name="o_ps")
-            for g in range(TC):
-                nc.tensor.matmul_mx(
-                    out=o_ps[:],
-                    lhsT=e_wd[i][:, P * g : P * g + P].bitcast(FP8X4),
-                    lhsT_scale=e_sc[i][:, P * g : P * g + P],
-                    rhs=v_words[:, VD * g : VD * g + VD].bitcast(FP8X4),
-                    rhs_scale=v_scales[:, VD * g : VD * g + VD],
-                    start=(g == 0),
-                    stop=(g == TC - 1),
-                )
+        def store(i):
             o_sb = work.tile([P, VD], F32, tag="o_sb", bufs=3, name="o_sb")
-            nc.vector.tensor_scalar(out=o_sb[:], in0=o_ps[:], scalar1=rinv[i][:], scalar2=None, op0=ALU.mult)
+            nc.vector.tensor_scalar(out=o_sb[:], in0=o_ps[i][:], scalar1=rinv[i][:], scalar2=None, op0=ALU.mult)
             nc.sync.dma_start(out=out_view[:, i, :], in_=o_sb[:])
 
-        query_pair(0)
-        query_pair(1)
-        for c in range(TC):
-            key_chunk(c)
-            scores(0, c)
-        for c in range(TC):
-            scores(1, c)
+        norms()
+        k_transpose(0, 0)
+        k_transpose(0, 1)
+        q_transpose(0)
+        k_exit(0, 0, "S")
+        k_exit(0, 1, "S")
+        q_exit(0, "S")
+        k_quantise(0)
+        q_quantise(0)
+        k_transpose(1, 0)
+        k_transpose(1, 1)
+        k_exit(1, 0, "S")
+        k_exit(1, 1, "S")
+        k_quantise(1)
+        for c in range(2, TC):
+            k_transpose(c, 0)
+            k_transpose(c, 1)
+            score_pass(0, c - 2)
+            k_exit(c, 0, "S")
+            k_exit(c, 1, "S")
+            score_exit(0, c - 2)
+            k_quantise(c)
+        q_transpose(1)
+        for c in (TC - 2, TC - 1):
+            score_pass(0, c)
+            score_exit(0, c)
+        bias(0)
+        q_exit(1, "S")
+        q_quantise(1)
         for g in range(TC):
-            value_chunk(g)
-        for i in range(NT):
-            softmax(i)
-            if i + 2 < NT:
-                for c in range(TC):
-                    scores(i + 2, c)
-            if i == 0:
-                query_pair(2)
-                query_pair(3)
-            weighted_sum(i)
+            v_regroup(g)
+
+        for p in range(NT - 1):
+            if p == 1:
+                q_exit(2, "S")
+                q_exit(3, "S")
+            if p >= 2:
+                for h in range(3):
+                    e_exit(p - 2, h, "S")
+            exponential(p, 0, 1)
+            for c in range(TC):
+                score_pass(p + 1, c)
+                if p >= 3:
+                    value_pass(p - 3, c)
+                score_exit(p + 1, c)
+            bias(p + 1)
+            if p >= 1:
+                for h in range(3):
+                    e_transpose(p - 1, h)
+            if p == 0:
+                q_transpose(2)
+                q_transpose(3)
+            if p == 1:
+                q_quantise(2)
+                q_quantise(3)
+            if p < 3:
+                v_quantise(2 * p)
+                v_quantise(2 * p + 1)
+            if p >= 2:
+                for h in range(3):
+                    e_quantise(p - 2, h)
+                row_scale(p - 2, 1)
+            if p >= 3:
+                store(p - 3)
+
+        for h in range(3):
+            e_transpose(6, h)
+        for h in range(3):
+            e_exit(5, h, "S")
+        for g in range(TC):
+            value_pass(4, g)
+        exponential(7, 0, 3)
+        for h in range(3):
+            e_exit(6, h, "V")
+        exponential(7, 1, 3)
+        e_transpose(7, 0)
+        store(4)
+        for h in range(3):
+            e_quantise(5, h)
+        row_scale(5, 1)
+        exponential(7, 2, 3)
+        e_transpose(7, 1)
+        for g in range(TC):
+            value_pass(5, g)
+        for h in range(3):
+            e_quantise(6, h)
+        row_scale(6, 1)
+        e_exit(7, 0, "V")
+        e_transpose(7, 2)
+        for g in range(TC):
+            value_pass(6, g)
+        e_exit(7, 1, "S")
+        e_quantise(7, 0)
+        store(5)
+        e_exit(7, 2, "S")
+        e_quantise(7, 1)
+        row_scale(7, 3)
+        for g in range(4):
+            value_pass(7, g)
+        store(6)
+        e_quantise(7, 2)
+        value_pass(7, 4)
+        value_pass(7, 5)
+        store(7)

@@ -20,9 +20,6 @@ SCALE = 6.25
 EPS = 1e-12
 FLOPS = 2 * N * T * QK + 2 * N * T * VD
 
-GPSIMD_TILES = 5
-SS_COL = {0: 0, 1: 1, 4: 2, 5: 3, 2: 4, 3: 5, 6: 6, 7: 7}
-
 
 def tile_contextrcnn_pb_kernel(tc, q_emb, keys, values, out):
     nc = tc.nc
@@ -40,18 +37,20 @@ def tile_contextrcnn_pb_kernel(tc, q_emb, keys, values, out):
 
         q_raw = keep.tile([P, NT, QK], BF16, name="q_raw")
         q_view = q_emb.rearrange("(p i) k -> p i k", i=NT)
-        for h in range(2):
-            nc.sync.dma_start(out=q_raw[:, 4 * h : 4 * h + 4, :], in_=q_view[:, 4 * h : 4 * h + 4, :])
         k_raw = []
-        for c in range(TC):
-            kr = keep.tile([P, 4, QK], BF16, name="k_raw%d" % c)
-            nc.sync.dma_start(out=kr[:], in_=keys[512 * c : 512 * c + 512, :].rearrange("(p a) k -> p a k", a=4))
-            k_raw.append(kr)
         v_raw = []
-        for g in range(TC):
-            vr = keep.tile([P, 4, VD], BF16, name="v_raw%d" % g)
-            nc.sync.dma_start(out=vr[:], in_=values[512 * g : 512 * g + 512, :].rearrange("(p j) w -> p j w", j=4))
-            v_raw.append(vr)
+
+        def load():
+            for h in range(2):
+                nc.sync.dma_start(out=q_raw[:, 4 * h : 4 * h + 4, :], in_=q_view[:, 4 * h : 4 * h + 4, :])
+            for c in range(TC):
+                kr = keep.tile([P, 4, QK], BF16, name="k_raw%d" % c)
+                nc.sync.dma_start(out=kr[:], in_=keys[512 * c : 512 * c + 512, :].rearrange("(p a) k -> p a k", a=4))
+                k_raw.append(kr)
+            for g in range(TC):
+                vr = keep.tile([P, 4, VD], BF16, name="v_raw%d" % g)
+                nc.sync.dma_start(out=vr[:], in_=values[512 * g : 512 * g + 512, :].rearrange("(p j) w -> p j w", j=4))
+                v_raw.append(vr)
 
         ident_bf = keep.tile([P, P], BF16, name="ident_bf")
         make_identity(nc, ident_bf[:])
@@ -60,10 +59,14 @@ def tile_contextrcnn_pb_kernel(tc, q_emb, keys, values, out):
         one = keep.tile([P, 1], F32, name="one")
         nc.vector.memset(one[:], 1.0)
         warm = keep.tile([P, 2], F32, name="warm")
-        nc.scalar.activation(out=warm[:, 0:1], in_=one[:], func=ACT.Sqrt)
 
-        ss_s = keep.tile([P, 4], F32, name="ss_s")
-        ss_v = keep.tile([P, 4], F32, name="ss_v")
+        def table(which):
+            if which == "Sqrt":
+                nc.scalar.activation(out=warm[:, 0:1], in_=one[:], func=ACT.Sqrt)
+            else:
+                nc.scalar.activation(out=warm[:, 1:2], in_=one[:], func=ACT.Exp)
+
+        ss = keep.tile([P, NT, 8], F32, name="ss")
         nrm = keep.tile([P, NT], F32, name="nrm")
         nrm_c = keep.tile([P, NT], F32, name="nrm_c")
         rn = keep.tile([P, NT], F32, name="rn")
@@ -72,24 +75,29 @@ def tile_contextrcnn_pb_kernel(tc, q_emb, keys, values, out):
         q_scales = keep.tile([P, NT * P], U8, name="q_scales", align_bytes=64)
         q_ps, q_grp = {}, {}
 
-        def norms():
-            for i in (0, 1, 4, 5):
+        def sumsq(i, engine):
+            if engine == "S":
                 sq = work.tile([P, QK], BF16, tag="sq", name="sq")
-                nc.scalar.activation(out=sq[:], in_=q_raw[:, i, :], func=ACT.Square, accum_out=ss_s[:, SS_COL[i] : SS_COL[i] + 1])
-            for i in (2, 3, 6, 7):
+                nc.scalar.activation(out=sq[:], in_=q_raw[:, i, :], func=ACT.Square, accum_out=ss[:, i, 0:1])
+            else:
                 sqf = work.tile([P, QK], F32, tag="sqf", name="sqf")
                 nc.vector.scalar_tensor_tensor(out=sqf[:], in0=q_raw[:, i, :], scalar=1.0, in1=q_raw[:, i, :], op0=ALU.mult, op1=ALU.mult,
-                                               accum_out=ss_v[:, SS_COL[i] - 4 : SS_COL[i] - 3])
-            nc.scalar.activation(out=nrm[:, 0:4], in_=ss_s[:], func=ACT.Sqrt)
-            nc.scalar.activation(out=nrm[:, 4:8], in_=ss_v[:], func=ACT.Sqrt)
-            nc.scalar.activation(out=warm[:, 1:2], in_=one[:], func=ACT.Exp)
-            nc.vector.tensor_scalar_max(out=nrm_c[:], in0=nrm[:], scalar1=EPS)
-            nc.vector.reciprocal(out=rn[:], in_=nrm_c[:])
-            for i in range(NT):
-                nc.vector.tensor_scalar(out=qn[:, i, :], in0=q_raw[:, i, :], scalar1=rn[:, SS_COL[i] : SS_COL[i] + 1], scalar2=None, op0=ALU.mult)
+                                               accum_out=ss[:, i, 0:1])
+
+        def norm_sqrt(h):
+            nc.scalar.activation(out=nrm[:, 4 * h : 4 * h + 4], in_=ss[:, 4 * h : 4 * h + 4, 0], func=ACT.Sqrt)
+
+        def norm_floor(h):
+            nc.vector.tensor_scalar_max(out=nrm_c[:, 4 * h : 4 * h + 4], in0=nrm[:, 4 * h : 4 * h + 4], scalar1=EPS)
+
+        def norm_recip(h):
+            nc.vector.reciprocal(out=rn[:, 4 * h : 4 * h + 4], in_=nrm_c[:, 4 * h : 4 * h + 4])
+
+        def scale(i):
+            nc.vector.tensor_scalar(out=qn[:, i, :], in0=q_raw[:, i, :], scalar1=rn[:, i : i + 1], scalar2=None, op0=ALU.mult)
 
         def q_transpose(b):
-            q_ps[b] = psum.tile([P, 2, 4, P], BF16, tag="t", bufs=3, name="qt")
+            q_ps[b] = psum.tile([P, 2, 4, P], BF16, tag="o", bufs=2, name="qt")
             for ii in range(2):
                 src = qn[:, 2 * b + ii, :].rearrange("p (u m e) -> p u e m", u=2, e=2)
                 for u in range(2):
@@ -120,7 +128,7 @@ def tile_contextrcnn_pb_kernel(tc, q_emb, keys, values, out):
                     nc.tensor.transpose(k_ps[c, h][:, a2, u, :], kw[:, col : col + 128], ident_f[:])
 
         def k_exit(c, h, engine):
-            if h == 0:
+            if c not in k_grp:
                 k_grp[c] = work.tile([P, 2048], BF16, tag="k_grp", align_bytes=64, name="k_grp")
             gw = k_grp[c][:].bitcast(F32).rearrange("p (a t u) -> p a t u", a=4, u=2)
             copy_on(engine, gw[:, 2 * h : 2 * h + 2, :, :], k_ps[c, h][:].rearrange("p a u t -> p a t u"))
@@ -136,12 +144,15 @@ def tile_contextrcnn_pb_kernel(tc, q_emb, keys, values, out):
         v_scales = keep.tile([P, TC * VD], U8, name="v_scales", align_bytes=64)
         v_grp = {}
 
-        def v_regroup(g):
+        def v_regroup(g, engine):
             v_grp[g] = work.tile([P, VD, 4], BF16, tag="v_grp", bufs=TC, align_bytes=64, name="v_grp")
-            for half in range(2):
-                w = slice(256 * half, 256 * half + 256)
-                nc.gpsimd.tensor_scalar(out=v_grp[g][:, w, :], in0=v_raw[g][:, :, w].rearrange("p t w -> p w t"),
-                                        scalar1=1.0, scalar2=0.0, op0=ALU.mult, op1=ALU.add)
+            if engine == "G":
+                for half in range(2):
+                    w = slice(256 * half, 256 * half + 256)
+                    nc.gpsimd.tensor_scalar(out=v_grp[g][:, w, :], in0=v_raw[g][:, :, w].rearrange("p t w -> p w t"),
+                                            scalar1=1.0, scalar2=0.0, op0=ALU.mult, op1=ALU.add)
+            else:
+                copy_on(engine, v_grp[g][:].rearrange("p (c i) t -> p c t i", i=4), v_raw[g][:].rearrange("p t (c i) -> p c t i", i=4))
 
         def v_quantise(g):
             nc.vector.quantize_mx(
@@ -165,7 +176,7 @@ def tile_contextrcnn_pb_kernel(tc, q_emb, keys, values, out):
             )
 
         def score_exit(i, c):
-            if c == 0:
+            if i not in s_sb:
                 s_sb[i] = work.tile([P, T], F32, tag="s_sb", bufs=2, name="s_sb")
                 mins[i] = work.tile([P, TC], F32, tag="mins", bufs=3, name="mins")
             nc.vector.tensor_scalar(
@@ -177,38 +188,41 @@ def tile_contextrcnn_pb_kernel(tc, q_emb, keys, values, out):
             nbias[i] = work.tile([P, 1], F32, tag="nbias", bufs=3, name="nbias")
             nc.vector.tensor_reduce(out=nbias[i][:], in_=mins[i][:], axis=AX.X, op=ALU.min)
 
-        def exponential(i, piece, pieces):
-            if piece == 0:
+        def exponential(i, c0, c1):
+            if i not in e_sb:
                 e_sb[i] = work.tile([P, T], BF16, tag="e_sb", bufs=2, name="e_sb")
-                rsum[i] = work.tile([P, pieces], F32, tag="rsum", bufs=5, name="rsum")
-            width = T // pieces
-            cols = slice(width * piece, width * piece + width)
+                rsum[i] = work.tile([P, TC // (c1 - c0)], F32, tag="rsum", bufs=5, name="rsum")
+            cols = slice(512 * c0, 512 * c1)
+            piece = c0 // (c1 - c0)
             nc.scalar.activation(out=e_sb[i][:, cols], in_=s_sb[i][:, cols], func=ACT.Exp, bias=nbias[i][:], scale=-1.0,
                                  accum_out=rsum[i][:, piece : piece + 1])
 
-        def e_transpose(i, h):
-            e_ps[i, h] = psum.tile([P, 2, 4, P], BF16, tag="t", bufs=3, name="et")
+        def e_transpose(i, h, tag):
+            e_ps[i, h] = psum.tile([P, 2, 4, P], BF16, tag=tag, bufs=3, name="et")
             for gg in range(2):
                 for j in range(4):
                     col = 1024 * h + 512 * gg + 128 * j
                     nc.tensor.transpose(e_ps[i, h][:, gg, j, :], e_sb[i][:, col : col + 128], ident_bf[:])
 
-        def e_exit(i, h, engine):
+        def e_exit(i, h, engine, via_gpsimd):
             if i not in e_grp:
                 e_grp[i] = work.tile([P, T], BF16, tag="e_grp", bufs=2, align_bytes=64, name="e_grp")
             cols = slice(1024 * h, 1024 * h + 1024)
-            dst = e_grp[i][:, cols].rearrange("p (g n j) -> p g n j", g=2, j=4)
-            if i < GPSIMD_TILES:
+            if via_gpsimd:
                 if i not in e_t:
                     e_t[i] = work.tile([P, T], BF16, tag="e_t", bufs=2, name="e_t")
                 copy_on(engine, e_t[i][:, cols], e_ps[i, h][:].rearrange("p g j n -> p (g j n)"))
-                nc.gpsimd.tensor_scalar(out=dst, in0=e_t[i][:, cols].rearrange("p (g j n) -> p g n j", g=2, j=4),
-                                        scalar1=1.0, scalar2=0.0, op0=ALU.mult, op1=ALU.add)
             else:
-                copy_on(engine, dst, e_ps[i, h][:].rearrange("p g j n -> p g n j"))
+                copy_on(engine, e_grp[i][:, cols].rearrange("p (g n j) -> p g n j", g=2, j=4), e_ps[i, h][:].rearrange("p g j n -> p g n j"))
+
+        def e_regroup(i, h):
+            cols = slice(1024 * h, 1024 * h + 1024)
+            nc.gpsimd.tensor_scalar(out=e_grp[i][:, cols].rearrange("p (g n j) -> p g n j", g=2, j=4),
+                                    in0=e_t[i][:, cols].rearrange("p (g j n) -> p g n j", g=2, j=4),
+                                    scalar1=1.0, scalar2=0.0, op0=ALU.mult, op1=ALU.add)
 
         def e_quantise(i, h):
-            if h == 0:
+            if i not in e_wd:
                 e_wd[i] = work.tile([P, T // 4], U32, tag="e_wd", bufs=3, align_bytes=64, name="e_wd")
                 e_sc[i] = work.tile([P, T // 4], U8, tag="e_sc", bufs=3, align_bytes=64, name="e_sc")
             nc.vector.quantize_mx(
@@ -217,9 +231,9 @@ def tile_contextrcnn_pb_kernel(tc, q_emb, keys, values, out):
                 in_=e_grp[i][:, 1024 * h : 1024 * h + 1024],
             )
 
-        def row_scale(i, pieces):
+        def row_scale(i):
             rinv[i] = work.tile([P, 1], F32, tag="rinv", bufs=4, name="rinv")
-            if pieces == 1:
+            if rsum[i].shape[1] == 1:
                 nc.vector.reciprocal(out=rinv[i][:], in_=rsum[i][:])
             else:
                 tot = work.tile([P, 1], F32, tag="tot", name="tot")
@@ -241,112 +255,358 @@ def tile_contextrcnn_pb_kernel(tc, q_emb, keys, values, out):
 
         out_view = out.rearrange("(p i) d -> p i d", i=NT)
 
-        def store(i):
+        def store(i, engine):
             o_sb = work.tile([P, VD], F32, tag="o_sb", bufs=3, name="o_sb")
-            nc.vector.tensor_scalar(out=o_sb[:], in0=o_ps[i][:], scalar1=rinv[i][:], scalar2=None, op0=ALU.mult)
+            if engine == "V":
+                nc.vector.tensor_scalar(out=o_sb[:], in0=o_ps[i][:], scalar1=rinv[i][:], scalar2=None, op0=ALU.mult)
+            else:
+                nc.scalar.activation(out=o_sb[:], in_=o_ps[i][:], func=ACT.Copy, scale=rinv[i][:])
             nc.sync.dma_start(out=out_view[:, i, :], in_=o_sb[:])
 
-        norms()
-        k_transpose(0, 0)
-        k_transpose(0, 1)
-        q_transpose(0)
-        k_exit(0, 0, "S")
-        k_exit(0, 1, "S")
-        q_exit(0, "S")
-        k_quantise(0)
-        q_quantise(0)
+        load()
+        sumsq(3, "V")
+        table("Sqrt")
+        sumsq(2, "V")
+        sumsq(6, "V")
+        sumsq(1, "S")
+        sumsq(0, "S")
         k_transpose(1, 0)
+        sumsq(7, "V")
+        v_regroup(4, "G")
+        sumsq(4, "S")
+        norm_sqrt(0)
+        k_transpose(0, 0)
+        sumsq(5, "S")
+        norm_floor(0)
+        norm_recip(0)
+        k_transpose(0, 1)
+        scale(1)
+        v_regroup(2, "G")
+        scale(0)
+        q_transpose(0)
+        scale(2)
+        v_regroup(5, "G")
+        scale(3)
+        norm_sqrt(1)
+        table("Exp")
+        k_exit(0, 1, "S")
+        norm_floor(1)
+        norm_recip(1)
+        scale(6)
+        k_exit(1, 0, "V")
+        k_exit(0, 0, "V")
+        scale(5)
+        k_quantise(0)
+        q_transpose(1)
+        q_exit(0, "S")
         k_transpose(1, 1)
-        k_exit(1, 0, "S")
+        k_transpose(2, 0)
+        q_quantise(0)
+        k_transpose(2, 1)
+        k_transpose(3, 0)
         k_exit(1, 1, "S")
         k_quantise(1)
-        for c in range(2, TC):
-            k_transpose(c, 0)
-            k_transpose(c, 1)
-            score_pass(0, c - 2)
-            k_exit(c, 0, "S")
-            k_exit(c, 1, "S")
-            score_exit(0, c - 2)
-            k_quantise(c)
-        q_transpose(1)
-        for c in (TC - 2, TC - 1):
-            score_pass(0, c)
-            score_exit(0, c)
-        bias(0)
+        k_exit(2, 0, "S")
+        k_exit(2, 1, "S")
+        scale(4)
+        k_exit(3, 0, "S")
+        score_pass(0, 0)
+        k_transpose(3, 1)
+        k_quantise(2)
+        score_pass(0, 1)
+        score_exit(0, 0)
+        k_exit(3, 1, "S")
+        v_regroup(3, "G")
+        scale(7)
+        k_transpose(4, 0)
+        k_quantise(3)
+        k_exit(4, 0, "S")
+        k_transpose(4, 1)
+        score_pass(0, 2)
+        k_transpose(5, 0)
+        k_exit(4, 1, "S")
+        score_exit(0, 2)
+        k_quantise(4)
+        k_transpose(5, 1)
+        score_exit(0, 1)
+        score_pass(0, 3)
+        k_exit(5, 0, "S")
+        score_pass(0, 4)
+        k_exit(5, 1, "S")
+        k_quantise(5)
+        v_regroup(0, "S")
+        score_exit(0, 3)
+        score_exit(0, 4)
+        score_pass(0, 5)
+        score_exit(0, 5)
         q_exit(1, "S")
+        bias(0)
         q_quantise(1)
-        for g in range(TC):
-            v_regroup(g)
-
-        for p in range(NT - 1):
-            if p == 1:
-                q_exit(2, "S")
-                q_exit(3, "S")
-            if p >= 2:
-                for h in range(3):
-                    e_exit(p - 2, h, "S")
-            exponential(p, 0, 1)
-            for c in range(TC):
-                score_pass(p + 1, c)
-                if p >= 3:
-                    value_pass(p - 3, c)
-                score_exit(p + 1, c)
-            bias(p + 1)
-            if p >= 1:
-                for h in range(3):
-                    e_transpose(p - 1, h)
-            if p == 0:
-                q_transpose(2)
-                q_transpose(3)
-            if p == 1:
-                q_quantise(2)
-                q_quantise(3)
-            if p < 3:
-                v_quantise(2 * p)
-                v_quantise(2 * p + 1)
-            if p >= 2:
-                for h in range(3):
-                    e_quantise(p - 2, h)
-                row_scale(p - 2, 1)
-            if p >= 3:
-                store(p - 3)
-
-        for h in range(3):
-            e_transpose(6, h)
-        for h in range(3):
-            e_exit(5, h, "S")
-        for g in range(TC):
-            value_pass(4, g)
-        exponential(7, 0, 3)
-        for h in range(3):
-            e_exit(6, h, "V")
-        exponential(7, 1, 3)
-        e_transpose(7, 0)
-        store(4)
-        for h in range(3):
-            e_quantise(5, h)
-        row_scale(5, 1)
-        exponential(7, 2, 3)
-        e_transpose(7, 1)
-        for g in range(TC):
-            value_pass(5, g)
-        for h in range(3):
-            e_quantise(6, h)
-        row_scale(6, 1)
-        e_exit(7, 0, "V")
-        e_transpose(7, 2)
-        for g in range(TC):
-            value_pass(6, g)
-        e_exit(7, 1, "S")
+        exponential(0, 0, 6)
+        v_regroup(1, "S")
+        score_pass(1, 0)
+        score_exit(1, 0)
+        score_pass(1, 1)
+        score_exit(1, 1)
+        score_pass(1, 2)
+        score_exit(1, 2)
+        score_pass(1, 3)
+        score_exit(1, 3)
+        score_pass(1, 4)
+        score_exit(1, 4)
+        score_pass(1, 5)
+        score_exit(1, 5)
+        bias(1)
+        q_transpose(2)
+        q_transpose(3)
+        v_quantise(0)
+        v_quantise(2)
+        q_exit(2, "S")
+        q_exit(3, "S")
+        exponential(1, 0, 6)
+        score_pass(2, 0)
+        score_exit(2, 0)
+        score_pass(2, 1)
+        score_exit(2, 1)
+        score_pass(2, 2)
+        score_exit(2, 2)
+        score_pass(2, 3)
+        score_exit(2, 3)
+        score_pass(2, 4)
+        score_exit(2, 4)
+        score_pass(2, 5)
+        score_exit(2, 5)
+        bias(2)
+        e_transpose(0, 0, "t")
+        e_transpose(0, 1, "t")
+        e_transpose(0, 2, "t")
+        q_quantise(2)
+        q_quantise(3)
+        v_quantise(1)
+        v_quantise(3)
+        e_exit(0, 0, "S", True)
+        e_regroup(0, 0)
+        e_exit(0, 1, "S", True)
+        e_regroup(0, 1)
+        e_exit(0, 2, "S", True)
+        e_regroup(0, 2)
+        exponential(2, 0, 6)
+        score_pass(3, 0)
+        score_exit(3, 0)
+        score_pass(3, 1)
+        score_exit(3, 1)
+        score_pass(3, 2)
+        score_exit(3, 2)
+        score_pass(3, 3)
+        score_exit(3, 3)
+        score_pass(3, 4)
+        score_exit(3, 4)
+        score_pass(3, 5)
+        score_exit(3, 5)
+        bias(3)
+        e_transpose(1, 0, "t")
+        e_transpose(1, 1, "t")
+        e_transpose(1, 2, "t")
+        v_quantise(4)
+        v_quantise(5)
+        e_quantise(0, 0)
+        e_quantise(0, 1)
+        e_quantise(0, 2)
+        row_scale(0)
+        e_exit(1, 0, "S", True)
+        e_regroup(1, 0)
+        e_exit(1, 1, "S", True)
+        e_regroup(1, 1)
+        e_exit(1, 2, "S", True)
+        e_regroup(1, 2)
+        exponential(3, 0, 6)
+        score_pass(4, 0)
+        value_pass(0, 0)
+        score_exit(4, 0)
+        score_pass(4, 1)
+        value_pass(0, 1)
+        score_exit(4, 1)
+        score_pass(4, 2)
+        value_pass(0, 2)
+        score_exit(4, 2)
+        score_pass(4, 3)
+        value_pass(0, 3)
+        score_exit(4, 3)
+        score_pass(4, 4)
+        value_pass(0, 4)
+        score_exit(4, 4)
+        score_pass(4, 5)
+        value_pass(0, 5)
+        score_exit(4, 5)
+        bias(4)
+        e_transpose(2, 0, "t")
+        e_transpose(2, 1, "t")
+        e_transpose(2, 2, "t")
+        e_quantise(1, 0)
+        e_quantise(1, 1)
+        e_quantise(1, 2)
+        row_scale(1)
+        store(0, "V")
+        e_exit(2, 0, "S", True)
+        e_regroup(2, 0)
+        e_exit(2, 1, "S", True)
+        e_regroup(2, 1)
+        e_exit(2, 2, "S", True)
+        e_regroup(2, 2)
+        exponential(4, 0, 6)
+        score_pass(5, 0)
+        value_pass(1, 0)
+        score_exit(5, 0)
+        score_pass(5, 1)
+        value_pass(1, 1)
+        score_exit(5, 1)
+        score_pass(5, 2)
+        value_pass(1, 2)
+        score_exit(5, 2)
+        score_pass(5, 3)
+        value_pass(1, 3)
+        score_exit(5, 3)
+        score_pass(5, 4)
+        value_pass(1, 4)
+        score_exit(5, 4)
+        score_pass(5, 5)
+        value_pass(1, 5)
+        score_exit(5, 5)
+        bias(5)
+        e_transpose(3, 0, "t")
+        e_transpose(3, 1, "t")
+        e_transpose(3, 2, "t")
+        e_quantise(2, 0)
+        e_quantise(2, 1)
+        e_quantise(2, 2)
+        row_scale(2)
+        store(1, "V")
+        e_exit(3, 0, "S", True)
+        e_regroup(3, 0)
+        e_exit(3, 1, "S", True)
+        e_regroup(3, 1)
+        e_exit(3, 2, "S", True)
+        e_regroup(3, 2)
+        exponential(5, 0, 6)
+        score_pass(6, 0)
+        value_pass(2, 0)
+        score_exit(6, 0)
+        score_pass(6, 1)
+        value_pass(2, 1)
+        score_exit(6, 1)
+        score_pass(6, 2)
+        value_pass(2, 2)
+        score_exit(6, 2)
+        score_pass(6, 3)
+        value_pass(2, 3)
+        score_exit(6, 3)
+        score_pass(6, 4)
+        value_pass(2, 4)
+        score_exit(6, 4)
+        score_pass(6, 5)
+        value_pass(2, 5)
+        score_exit(6, 5)
+        bias(6)
+        e_transpose(4, 0, "t")
+        e_transpose(4, 1, "t")
+        e_transpose(4, 2, "t")
+        e_quantise(3, 0)
+        e_quantise(3, 1)
+        e_quantise(3, 2)
+        row_scale(3)
+        store(2, "V")
+        e_exit(4, 0, "S", True)
+        e_regroup(4, 0)
+        e_exit(4, 1, "S", True)
+        e_regroup(4, 1)
+        e_exit(4, 2, "S", True)
+        e_regroup(4, 2)
+        exponential(6, 0, 6)
+        score_pass(7, 0)
+        value_pass(3, 0)
+        score_exit(7, 0)
+        score_pass(7, 1)
+        value_pass(3, 1)
+        score_exit(7, 1)
+        score_pass(7, 2)
+        value_pass(3, 2)
+        score_exit(7, 2)
+        score_pass(7, 3)
+        value_pass(3, 3)
+        score_exit(7, 3)
+        score_pass(7, 4)
+        value_pass(3, 4)
+        score_exit(7, 4)
+        score_pass(7, 5)
+        value_pass(3, 5)
+        score_exit(7, 5)
+        bias(7)
+        e_transpose(5, 0, "t")
+        e_transpose(5, 1, "t")
+        e_transpose(5, 2, "t")
+        e_quantise(4, 0)
+        e_quantise(4, 1)
+        e_quantise(4, 2)
+        row_scale(4)
+        store(3, "V")
+        e_exit(5, 0, "V", True)
+        e_exit(5, 1, "S", True)
+        value_pass(4, 0)
+        e_exit(5, 2, "V", True)
+        value_pass(4, 1)
+        value_pass(4, 2)
+        exponential(7, 2, 4)
+        exponential(7, 4, 6)
+        value_pass(4, 3)
+        value_pass(4, 4)
+        value_pass(4, 5)
+        e_regroup(5, 1)
+        e_transpose(6, 0, "t")
+        e_transpose(6, 1, "t")
+        e_transpose(7, 1, "s")
+        store(4, "V")
+        e_exit(6, 0, "V", False)
+        exponential(7, 0, 2)
+        e_regroup(5, 0)
+        row_scale(5)
+        e_exit(6, 1, "S", False)
+        e_regroup(5, 2)
+        e_quantise(5, 0)
+        e_quantise(5, 1)
+        e_transpose(6, 2, "t")
+        e_quantise(5, 2)
+        e_transpose(7, 0, "s")
+        e_transpose(7, 2, "s")
+        row_scale(7)
+        value_pass(5, 0)
+        value_pass(5, 1)
+        value_pass(5, 2)
+        value_pass(5, 3)
+        e_quantise(6, 1)
+        e_exit(6, 2, "S", False)
+        value_pass(5, 4)
+        e_quantise(6, 0)
+        value_pass(5, 5)
+        value_pass(6, 0)
+        value_pass(6, 1)
+        row_scale(6)
+        value_pass(6, 2)
+        value_pass(6, 3)
+        e_quantise(6, 2)
+        value_pass(6, 4)
+        e_exit(7, 2, "V", False)
+        value_pass(6, 5)
+        e_exit(7, 0, "S", False)
+        e_exit(7, 1, "S", False)
         e_quantise(7, 0)
-        store(5)
-        e_exit(7, 2, "S")
         e_quantise(7, 1)
-        row_scale(7, 3)
-        for g in range(4):
-            value_pass(7, g)
-        store(6)
+        value_pass(7, 0)
+        value_pass(7, 1)
+        value_pass(7, 2)
+        value_pass(7, 3)
         e_quantise(7, 2)
         value_pass(7, 4)
+        store(5, "S")
         value_pass(7, 5)
-        store(7)
+        store(6, "V")
+        store(7, "S")

@@ -264,82 +264,82 @@ def tile_contextrcnn_pb_kernel(tc, q_emb, keys, values, out):
             nc.sync.dma_start(out=out_view[:, i, :], in_=o_sb[:])
 
         load()
-        sumsq(3, "V")
         table("Sqrt")
-        sumsq(2, "V")
-        sumsq(6, "V")
+        sumsq(3, "V")
         sumsq(1, "S")
         sumsq(0, "S")
-        k_transpose(1, 0)
-        sumsq(7, "V")
-        v_regroup(4, "G")
+        sumsq(2, "V")
         sumsq(4, "S")
+        sumsq(6, "V")
+        sumsq(7, "V")
         norm_sqrt(0)
-        k_transpose(0, 0)
-        sumsq(5, "S")
         norm_floor(0)
         norm_recip(0)
         k_transpose(0, 1)
         scale(1)
-        v_regroup(2, "G")
+        v_regroup(4, "G")
+        k_transpose(0, 0)
         scale(0)
+        k_transpose(1, 0)
+        sumsq(5, "S")
         q_transpose(0)
-        scale(2)
-        v_regroup(5, "G")
-        scale(3)
-        norm_sqrt(1)
-        table("Exp")
-        k_exit(0, 1, "S")
-        norm_floor(1)
-        norm_recip(1)
-        scale(6)
-        k_exit(1, 0, "V")
         k_exit(0, 0, "V")
-        scale(5)
+        k_exit(0, 1, "V")
+        norm_sqrt(1)
         k_quantise(0)
-        q_transpose(1)
-        q_exit(0, "S")
         k_transpose(1, 1)
+        scale(3)
         k_transpose(2, 0)
+        norm_floor(1)
+        k_exit(1, 0, "V")
+        norm_recip(1)
+        scale(2)
+        table("Exp")
+        q_exit(0, "S")
+        scale(6)
         q_quantise(0)
-        k_transpose(2, 1)
-        k_transpose(3, 0)
         k_exit(1, 1, "S")
-        k_quantise(1)
+        k_transpose(2, 1)
+        scale(7)
         k_exit(2, 0, "S")
+        k_quantise(1)
+        k_transpose(3, 0)
         k_exit(2, 1, "S")
-        scale(4)
-        k_exit(3, 0, "S")
         score_pass(0, 0)
         k_transpose(3, 1)
+        v_regroup(2, "G")
+        k_exit(3, 1, "S")
+        v_regroup(5, "G")
+        k_transpose(4, 0)
+        k_transpose(4, 1)
+        scale(5)
+        v_regroup(3, "G")
+        k_exit(3, 0, "V")
         k_quantise(2)
+        k_exit(4, 0, "S")
         score_pass(0, 1)
         score_exit(0, 0)
-        k_exit(3, 1, "S")
-        v_regroup(3, "G")
-        scale(7)
-        k_transpose(4, 0)
-        k_quantise(3)
-        k_exit(4, 0, "S")
-        k_transpose(4, 1)
         score_pass(0, 2)
-        k_transpose(5, 0)
-        k_exit(4, 1, "S")
+        k_quantise(3)
         score_exit(0, 2)
+        k_exit(4, 1, "S")
         k_quantise(4)
-        k_transpose(5, 1)
         score_exit(0, 1)
-        score_pass(0, 3)
+        k_transpose(5, 0)
+        k_transpose(5, 1)
+        q_transpose(1)
         k_exit(5, 0, "S")
-        score_pass(0, 4)
         k_exit(5, 1, "S")
+        score_pass(0, 4)
+        scale(4)
+        q_exit(1, "S")
+        score_pass(0, 3)
         k_quantise(5)
-        v_regroup(0, "S")
+        score_pass(0, 5)
         score_exit(0, 3)
         score_exit(0, 4)
-        score_pass(0, 5)
         score_exit(0, 5)
-        q_exit(1, "S")
+        v_regroup(0, "S")
         bias(0)
         q_quantise(1)
         exponential(0, 0, 6)
@@ -384,7 +384,7 @@ def tile_contextrcnn_pb_kernel(tc, q_emb, keys, values, out):
         q_quantise(3)
         v_quantise(1)
         v_quantise(3)
-        e_exit(0, 0, "S", True)
+        e_exit(0, 0, "V", True)
         e_regroup(0, 0)
         e_exit(0, 1, "S", True)
         e_regroup(0, 1)
@@ -446,12 +446,12 @@ def tile_contextrcnn_pb_kernel(tc, q_emb, keys, values, out):
         e_quantise(1, 1)
         e_quantise(1, 2)
         row_scale(1)
-        store(0, "V")
+        store(0, "S")
         e_exit(2, 0, "S", True)
         e_regroup(2, 0)
         e_exit(2, 1, "S", True)
         e_regroup(2, 1)
-        e_exit(2, 2, "S", True)
+        e_exit(2, 2, "V", True)
         e_regroup(2, 2)
         exponential(4, 0, 6)
         score_pass(5, 0)
@@ -550,63 +550,63 @@ def tile_contextrcnn_pb_kernel(tc, q_emb, keys, values, out):
         row_scale(4)
         store(3, "V")
         e_exit(5, 0, "V", True)
-        e_exit(5, 1, "S", True)
         value_pass(4, 0)
+        e_exit(5, 1, "S", True)
+        e_regroup(5, 1)
+        e_regroup(5, 0)
         e_exit(5, 2, "V", True)
+        e_regroup(5, 2)
         value_pass(4, 1)
         value_pass(4, 2)
         exponential(7, 2, 4)
-        exponential(7, 4, 6)
+        exponential(7, 0, 2)
         value_pass(4, 3)
         value_pass(4, 4)
         value_pass(4, 5)
-        e_regroup(5, 1)
         e_transpose(6, 0, "t")
+        exponential(7, 4, 6)
+        store(4, "V")
         e_transpose(6, 1, "t")
         e_transpose(7, 1, "s")
-        store(4, "V")
-        e_exit(6, 0, "V", False)
-        exponential(7, 0, 2)
-        e_regroup(5, 0)
-        row_scale(5)
-        e_exit(6, 1, "S", False)
-        e_regroup(5, 2)
-        e_quantise(5, 0)
-        e_quantise(5, 1)
         e_transpose(6, 2, "t")
-        e_quantise(5, 2)
+        e_exit(6, 0, "V", False)
+        e_exit(6, 1, "V", False)
+        e_quantise(5, 0)
         e_transpose(7, 0, "s")
+        e_quantise(5, 2)
         e_transpose(7, 2, "s")
-        row_scale(7)
+        e_quantise(5, 1)
         value_pass(5, 0)
         value_pass(5, 1)
         value_pass(5, 2)
-        value_pass(5, 3)
-        e_quantise(6, 1)
         e_exit(6, 2, "S", False)
-        value_pass(5, 4)
         e_quantise(6, 0)
+        value_pass(5, 3)
+        row_scale(5)
+        e_quantise(6, 1)
+        e_quantise(6, 2)
+        value_pass(5, 4)
+        e_exit(7, 0, "S", False)
+        e_exit(7, 2, "V", False)
         value_pass(5, 5)
         value_pass(6, 0)
         value_pass(6, 1)
-        row_scale(6)
+        e_exit(7, 1, "S", False)
+        store(5, "V")
         value_pass(6, 2)
         value_pass(6, 3)
-        e_quantise(6, 2)
-        value_pass(6, 4)
-        e_exit(7, 2, "V", False)
-        value_pass(6, 5)
-        e_exit(7, 0, "S", False)
-        e_exit(7, 1, "S", False)
         e_quantise(7, 0)
-        e_quantise(7, 1)
+        value_pass(6, 4)
+        value_pass(6, 5)
         value_pass(7, 0)
         value_pass(7, 1)
+        row_scale(7)
+        e_quantise(7, 1)
         value_pass(7, 2)
         value_pass(7, 3)
+        row_scale(6)
         e_quantise(7, 2)
         value_pass(7, 4)
-        store(5, "S")
         value_pass(7, 5)
         store(6, "V")
-        store(7, "S")
+        store(7, "V")

@@ -13,12 +13,21 @@ ACT = mybir.ActivationFunctionType
 AX = mybir.AxisListType
 
 P = 128
+PACK = 4
 N, T, QK, VD = 1024, 3072, 512, 512
-NT = N // P
-TC = T // 512
-SCALE = 6.25
-EPS = 1e-12
+CHUNK = P * PACK
+TILES = N // P
+CHUNKS = T // CHUNK
+BANK = 2 * CHUNK
+BANKS = T // BANK
+SOFTMAX_SCALE = 6.25
+NORM_FLOOR = 1e-12
 FLOPS = 2 * N * T * QK + 2 * N * T * VD
+
+GPSIMD_TILES = TILES - 2
+SCALAR_VALUE_CHUNKS = (0, 1)
+GPSIMD_VALUE_CHUNKS = (5, 2, 3, 4)
+VALUE_QUANTISE_ORDER = ((0, 5), (1, 2), (3, 4))
 
 
 def tile_contextrcnn_pb_kernel(tc, q_emb, keys, values, out):
@@ -26,7 +35,7 @@ def tile_contextrcnn_pb_kernel(tc, q_emb, keys, values, out):
     with ExitStack() as ctx:
         ctx.enter_context(tc.manual_schedule())
         keep = ctx.enter_context(tc.tile_pool(name="keep", bufs=1))
-        work = ctx.enter_context(tc.tile_pool(name="work", bufs=2))
+        ring = ctx.enter_context(tc.tile_pool(name="ring", bufs=2))
         psum = ctx.enter_context(tc.psum_pool(name="psum", bufs=1))
 
         def copy_on(engine, out_ap, in_ap):
@@ -35,22 +44,23 @@ def tile_contextrcnn_pb_kernel(tc, q_emb, keys, values, out):
             else:
                 nc.scalar.copy(out=out_ap, in_=in_ap)
 
-        q_raw = keep.tile([P, NT, QK], BF16, name="q_raw")
-        q_view = q_emb.rearrange("(p i) k -> p i k", i=NT)
+        q_raw = keep.tile([P, TILES, QK], BF16, name="q_raw")
         k_raw = []
         v_raw = []
 
         def load():
-            for h in range(2):
-                nc.sync.dma_start(out=q_raw[:, 4 * h : 4 * h + 4, :], in_=q_view[:, 4 * h : 4 * h + 4, :])
-            for c in range(TC):
-                kr = keep.tile([P, 4, QK], BF16, name="k_raw%d" % c)
-                nc.sync.dma_start(out=kr[:], in_=keys[512 * c : 512 * c + 512, :].rearrange("(p a) k -> p a k", a=4))
-                k_raw.append(kr)
-            for g in range(TC):
-                vr = keep.tile([P, 4, VD], BF16, name="v_raw%d" % g)
-                nc.sync.dma_start(out=vr[:], in_=values[512 * g : 512 * g + 512, :].rearrange("(p j) w -> p j w", j=4))
-                v_raw.append(vr)
+            q_view = q_emb.rearrange("(p i) k -> p i k", i=TILES)
+            for pair in range(TILES // 2):
+                tiles = slice(2 * pair, 2 * pair + 2)
+                nc.sync.dma_start(out=q_raw[:, tiles, :], in_=q_view[:, tiles, :])
+            for c in range(CHUNKS):
+                rows = keep.tile([P, PACK, QK], BF16, name="k_raw%d" % c)
+                nc.sync.dma_start(out=rows[:], in_=keys[CHUNK * c : CHUNK * (c + 1), :].rearrange("(p a) k -> p a k", a=PACK))
+                k_raw.append(rows)
+            for g in range(CHUNKS):
+                rows = keep.tile([P, PACK, VD], BF16, name="v_raw%d" % g)
+                nc.sync.dma_start(out=rows[:], in_=values[CHUNK * g : CHUNK * (g + 1), :].rearrange("(p j) w -> p j w", j=PACK))
+                v_raw.append(rows)
 
         ident_bf = keep.tile([P, P], BF16, name="ident_bf")
         make_identity(nc, ident_bf[:])
@@ -60,553 +70,328 @@ def tile_contextrcnn_pb_kernel(tc, q_emb, keys, values, out):
         nc.vector.memset(one[:], 1.0)
         warm = keep.tile([P, 2], F32, name="warm")
 
-        def table(which):
-            if which == "Sqrt":
-                nc.scalar.activation(out=warm[:, 0:1], in_=one[:], func=ACT.Sqrt)
-            else:
-                nc.scalar.activation(out=warm[:, 1:2], in_=one[:], func=ACT.Exp)
+        def load_table(func, column):
+            nc.scalar.activation(out=warm[:, column : column + 1], in_=one[:], func=func)
 
-        ss = keep.tile([P, NT, 8], F32, name="ss")
-        nrm = keep.tile([P, NT], F32, name="nrm")
-        nrm_c = keep.tile([P, NT], F32, name="nrm_c")
-        rn = keep.tile([P, NT], F32, name="rn")
-        qn = keep.tile([P, NT, QK], BF16, name="qn")
-        q_words = keep.tile([P, NT * P], U32, name="q_words", align_bytes=64)
-        q_scales = keep.tile([P, NT * P], U8, name="q_scales", align_bytes=64)
-        q_ps, q_grp = {}, {}
+        sumsq = keep.tile([P, TILES, 8], F32, name="sumsq")
+        norm = keep.tile([P, TILES], F32, name="norm")
+        norm_floored = keep.tile([P, TILES], F32, name="norm_floored")
+        inv_norm = keep.tile([P, TILES], F32, name="inv_norm")
+        q_hat = keep.tile([P, TILES, QK], BF16, name="q_hat")
+        q_codes = keep.tile([P, N], U32, name="q_codes", align_bytes=64)
+        q_scales = keep.tile([P, N], U8, name="q_scales", align_bytes=64)
+        q_flipped, q_grouped = {}, {}
 
-        def sumsq(i, engine):
+        def sum_squares(i, engine):
             if engine == "S":
-                sq = work.tile([P, QK], BF16, tag="sq", name="sq")
-                nc.scalar.activation(out=sq[:], in_=q_raw[:, i, :], func=ACT.Square, accum_out=ss[:, i, 0:1])
+                squares = ring.tile([P, QK], BF16, tag="squares_bf", name="squares_bf")
+                nc.scalar.activation(out=squares[:], in_=q_raw[:, i, :], func=ACT.Square, accum_out=sumsq[:, i, 0:1])
             else:
-                sqf = work.tile([P, QK], F32, tag="sqf", name="sqf")
-                nc.vector.scalar_tensor_tensor(out=sqf[:], in0=q_raw[:, i, :], scalar=1.0, in1=q_raw[:, i, :], op0=ALU.mult, op1=ALU.mult,
-                                               accum_out=ss[:, i, 0:1])
+                squares = ring.tile([P, QK], F32, tag="squares_f", name="squares_f")
+                nc.vector.scalar_tensor_tensor(out=squares[:], in0=q_raw[:, i, :], scalar=1.0, in1=q_raw[:, i, :],
+                                               op0=ALU.mult, op1=ALU.mult, accum_out=sumsq[:, i, 0:1])
+
+        def half(h):
+            return slice(TILES // 2 * h, TILES // 2 * (h + 1))
 
         def norm_sqrt(h):
-            nc.scalar.activation(out=nrm[:, 4 * h : 4 * h + 4], in_=ss[:, 4 * h : 4 * h + 4, 0], func=ACT.Sqrt)
+            nc.scalar.activation(out=norm[:, half(h)], in_=sumsq[:, half(h), 0], func=ACT.Sqrt)
 
-        def norm_floor(h):
-            nc.vector.tensor_scalar_max(out=nrm_c[:, 4 * h : 4 * h + 4], in0=nrm[:, 4 * h : 4 * h + 4], scalar1=EPS)
+        def norm_invert(h):
+            nc.vector.tensor_scalar_max(out=norm_floored[:, half(h)], in0=norm[:, half(h)], scalar1=NORM_FLOOR)
+            nc.vector.reciprocal(out=inv_norm[:, half(h)], in_=norm_floored[:, half(h)])
 
-        def norm_recip(h):
-            nc.vector.reciprocal(out=rn[:, 4 * h : 4 * h + 4], in_=nrm_c[:, 4 * h : 4 * h + 4])
+        def normalise(i):
+            nc.vector.tensor_scalar(out=q_hat[:, i, :], in0=q_raw[:, i, :], scalar1=inv_norm[:, i : i + 1], scalar2=None, op0=ALU.mult)
 
-        def scale(i):
-            nc.vector.tensor_scalar(out=qn[:, i, :], in0=q_raw[:, i, :], scalar1=rn[:, i : i + 1], scalar2=None, op0=ALU.mult)
-
-        def q_transpose(b):
-            q_ps[b] = psum.tile([P, 2, 4, P], BF16, tag="o", bufs=2, name="qt")
-            for ii in range(2):
-                src = qn[:, 2 * b + ii, :].rearrange("p (u m e) -> p u e m", u=2, e=2)
+        def q_transpose(pair):
+            q_flipped[pair] = psum.tile([P, 2, PACK, P], BF16, tag="out", bufs=2, name="q_flipped")
+            for i in range(2):
+                columns = q_hat[:, 2 * pair + i, :].rearrange("p (u m e) -> p u e m", u=2, e=2)
                 for u in range(2):
                     for e in range(2):
-                        nc.tensor.transpose(q_ps[b][:, ii, 2 * u + e, :], src[:, u, e, :], ident_bf[:])
+                        nc.tensor.transpose(q_flipped[pair][:, i, 2 * u + e, :], columns[:, u, e, :], ident_bf[:])
 
-        def q_exit(b, engine):
-            q_grp[b] = work.tile([P, 1024], BF16, tag="q_grp", align_bytes=64, name="q_grp")
-            copy_on(engine, q_grp[b][:].rearrange("p (i n t) -> p i n t", i=2, t=4), q_ps[b][:].rearrange("p i t n -> p i n t"))
+        def q_exit(pair, engine):
+            q_grouped[pair] = ring.tile([P, 2 * P * PACK], BF16, tag="q_grouped", align_bytes=64, name="q_grouped")
+            copy_on(engine, q_grouped[pair][:].rearrange("p (i n t) -> p i n t", i=2, t=PACK),
+                    q_flipped[pair][:].rearrange("p i t n -> p i n t"))
 
-        def q_quantise(b):
-            nc.vector.quantize_mx(
-                out=q_words[:, 256 * b : 256 * b + 256].bitcast(FP8X4),
-                scales=q_scales[:, 256 * b : 256 * b + 256],
-                in_=q_grp[b][:],
-            )
+        def q_quantise(pair):
+            columns = slice(2 * P * pair, 2 * P * (pair + 1))
+            nc.vector.quantize_mx(out=q_codes[:, columns].bitcast(FP8X4), scales=q_scales[:, columns], in_=q_grouped[pair][:])
 
-        k_words = keep.tile([P, T], U32, name="k_words", align_bytes=64)
+        k_codes = keep.tile([P, T], U32, name="k_codes", align_bytes=64)
         k_scales = keep.tile([P, T], U8, name="k_scales", align_bytes=64)
-        k_ps, k_grp = {}, {}
+        k_flipped, k_grouped = {}, {}
 
         def k_transpose(c, h):
-            kw = k_raw[c][:].rearrange("p a k -> p (a k)").bitcast(F32)
-            k_ps[c, h] = psum.tile([P, 2, 2, P], F32, tag="t", bufs=3, name="kt")
-            for a2 in range(2):
+            words = k_raw[c][:].rearrange("p a k -> p (a k)").bitcast(F32)
+            k_flipped[c, h] = psum.tile([P, 2, 2, P], F32, tag="flip", bufs=3, name="k_flipped")
+            for a in range(2):
                 for u in range(2):
-                    col = 256 * (2 * h + a2) + 128 * u
-                    nc.tensor.transpose(k_ps[c, h][:, a2, u, :], kw[:, col : col + 128], ident_f[:])
+                    first = QK // 2 * (2 * h + a) + P * u
+                    nc.tensor.transpose(k_flipped[c, h][:, a, u, :], words[:, first : first + P], ident_f[:])
 
         def k_exit(c, h, engine):
-            if c not in k_grp:
-                k_grp[c] = work.tile([P, 2048], BF16, tag="k_grp", align_bytes=64, name="k_grp")
-            gw = k_grp[c][:].bitcast(F32).rearrange("p (a t u) -> p a t u", a=4, u=2)
-            copy_on(engine, gw[:, 2 * h : 2 * h + 2, :, :], k_ps[c, h][:].rearrange("p a u t -> p a t u"))
+            if c not in k_grouped:
+                k_grouped[c] = ring.tile([P, CHUNK * PACK], BF16, tag="k_grouped", align_bytes=64, name="k_grouped")
+            words = k_grouped[c][:].bitcast(F32).rearrange("p (a t u) -> p a t u", a=PACK, u=2)
+            copy_on(engine, words[:, 2 * h : 2 * h + 2, :, :], k_flipped[c, h][:].rearrange("p a u t -> p a t u"))
 
         def k_quantise(c):
-            nc.vector.quantize_mx(
-                out=k_words[:, 512 * c : 512 * c + 512].bitcast(FP8X4),
-                scales=k_scales[:, 512 * c : 512 * c + 512],
-                in_=k_grp[c][:],
-            )
+            columns = slice(CHUNK * c, CHUNK * (c + 1))
+            nc.vector.quantize_mx(out=k_codes[:, columns].bitcast(FP8X4), scales=k_scales[:, columns], in_=k_grouped[c][:])
 
-        v_words = keep.tile([P, TC * VD], U32, name="v_words", align_bytes=64)
-        v_scales = keep.tile([P, TC * VD], U8, name="v_scales", align_bytes=64)
-        v_grp = {}
+        v_codes = keep.tile([P, CHUNKS * VD], U32, name="v_codes", align_bytes=64)
+        v_scales = keep.tile([P, CHUNKS * VD], U8, name="v_scales", align_bytes=64)
+        v_grouped = {}
 
         def v_regroup(g, engine):
-            v_grp[g] = work.tile([P, VD, 4], BF16, tag="v_grp", bufs=TC, align_bytes=64, name="v_grp")
+            v_grouped[g] = ring.tile([P, VD, PACK], BF16, tag="v_grouped", bufs=CHUNKS, align_bytes=64, name="v_grouped")
             if engine == "G":
-                for half in range(2):
-                    w = slice(256 * half, 256 * half + 256)
-                    nc.gpsimd.tensor_scalar(out=v_grp[g][:, w, :], in0=v_raw[g][:, :, w].rearrange("p t w -> p w t"),
+                for part in range(2):
+                    w = slice(VD // 2 * part, VD // 2 * (part + 1))
+                    nc.gpsimd.tensor_scalar(out=v_grouped[g][:, w, :], in0=v_raw[g][:, :, w].rearrange("p j w -> p w j"),
                                             scalar1=1.0, scalar2=0.0, op0=ALU.mult, op1=ALU.add)
             else:
-                copy_on(engine, v_grp[g][:].rearrange("p (c i) t -> p c t i", i=4), v_raw[g][:].rearrange("p t (c i) -> p c t i", i=4))
+                copy_on(engine, v_grouped[g][:].rearrange("p (c i) j -> p c j i", i=4), v_raw[g][:].rearrange("p j (c i) -> p c j i", i=4))
 
         def v_quantise(g):
-            nc.vector.quantize_mx(
-                out=v_words[:, VD * g : VD * g + VD].bitcast(FP8X4),
-                scales=v_scales[:, VD * g : VD * g + VD],
-                in_=v_grp[g][:].rearrange("p w t -> p (w t)"),
-            )
+            columns = slice(VD * g, VD * (g + 1))
+            nc.vector.quantize_mx(out=v_codes[:, columns].bitcast(FP8X4), scales=v_scales[:, columns],
+                                  in_=v_grouped[g][:].rearrange("p w j -> p (w j)"))
 
-        s_ps, s_sb, mins, nbias, e_sb, rsum, e_ps, e_t, e_grp, e_wd, e_sc, rinv, o_ps = {}, {}, {}, {}, {}, {}, {}, {}, {}, {}, {}, {}, {}
+        s_bank, s_neg, bank_min, exp_bias = {}, {}, {}, {}
+        e_rows, e_sum, e_flipped, e_plain, e_grouped, e_codes, e_scales = {}, {}, {}, {}, {}, {}, {}
+        inv_sum, o_bank = {}, {}
 
         def score_pass(i, c):
-            s_ps[i, c] = psum.tile([P, 512], F32, tag="s", bufs=3, name="s_ps")
+            s_bank[i, c] = psum.tile([P, CHUNK], F32, tag="score", bufs=3, name="s_bank")
             nc.tensor.matmul_mx(
-                out=s_ps[i, c][:],
-                lhsT=q_words[:, P * i : P * i + P].bitcast(FP8X4),
-                lhsT_scale=q_scales[:, P * i : P * i + P],
-                rhs=k_words[:, 512 * c : 512 * c + 512].bitcast(FP8X4),
-                rhs_scale=k_scales[:, 512 * c : 512 * c + 512],
+                out=s_bank[i, c][:],
+                lhsT=q_codes[:, P * i : P * (i + 1)].bitcast(FP8X4),
+                lhsT_scale=q_scales[:, P * i : P * (i + 1)],
+                rhs=k_codes[:, CHUNK * c : CHUNK * (c + 1)].bitcast(FP8X4),
+                rhs_scale=k_scales[:, CHUNK * c : CHUNK * (c + 1)],
                 start=True,
                 stop=True,
             )
 
         def score_exit(i, c):
-            if i not in s_sb:
-                s_sb[i] = work.tile([P, T], F32, tag="s_sb", bufs=2, name="s_sb")
-                mins[i] = work.tile([P, TC], F32, tag="mins", bufs=3, name="mins")
-            nc.vector.tensor_scalar(
-                out=s_sb[i][:, 512 * c : 512 * c + 512], in0=s_ps[i, c][:], scalar1=-SCALE, scalar2=None,
-                op0=ALU.mult, op1=ALU.min, accum_out=mins[i][:, c : c + 1],
-            )
+            if i not in s_neg:
+                s_neg[i] = ring.tile([P, T], F32, tag="s_neg", name="s_neg")
+                bank_min[i] = ring.tile([P, CHUNKS], F32, tag="bank_min", bufs=3, name="bank_min")
+            nc.vector.tensor_scalar(out=s_neg[i][:, CHUNK * c : CHUNK * (c + 1)], in0=s_bank[i, c][:], scalar1=-SOFTMAX_SCALE, scalar2=None,
+                                    op0=ALU.mult, op1=ALU.min, accum_out=bank_min[i][:, c : c + 1])
 
-        def bias(i):
-            nbias[i] = work.tile([P, 1], F32, tag="nbias", bufs=3, name="nbias")
-            nc.vector.tensor_reduce(out=nbias[i][:], in_=mins[i][:], axis=AX.X, op=ALU.min)
+        def row_bias(i):
+            exp_bias[i] = ring.tile([P, 1], F32, tag="exp_bias", bufs=3, name="exp_bias")
+            nc.vector.tensor_reduce(out=exp_bias[i][:], in_=bank_min[i][:], axis=AX.X, op=ALU.min)
 
-        def exponential(i, c0, c1):
-            if i not in e_sb:
-                e_sb[i] = work.tile([P, T], BF16, tag="e_sb", bufs=2, name="e_sb")
-                rsum[i] = work.tile([P, TC // (c1 - c0)], F32, tag="rsum", bufs=5, name="rsum")
-            cols = slice(512 * c0, 512 * c1)
-            piece = c0 // (c1 - c0)
-            nc.scalar.activation(out=e_sb[i][:, cols], in_=s_sb[i][:, cols], func=ACT.Exp, bias=nbias[i][:], scale=-1.0,
-                                 accum_out=rsum[i][:, piece : piece + 1])
+        def exponential(i, piece, pieces):
+            if i not in e_rows:
+                e_rows[i] = ring.tile([P, T], BF16, tag="e_rows", name="e_rows")
+                e_sum[i] = ring.tile([P, pieces], F32, tag="e_sum", bufs=5, name="e_sum")
+            columns = slice(T // pieces * piece, T // pieces * (piece + 1))
+            nc.scalar.activation(out=e_rows[i][:, columns], in_=s_neg[i][:, columns], func=ACT.Exp, bias=exp_bias[i][:], scale=-1.0,
+                                 accum_out=e_sum[i][:, piece : piece + 1])
 
-        def e_transpose(i, h, tag):
-            e_ps[i, h] = psum.tile([P, 2, 4, P], BF16, tag=tag, bufs=3, name="et")
-            for gg in range(2):
-                for j in range(4):
-                    col = 1024 * h + 512 * gg + 128 * j
-                    nc.tensor.transpose(e_ps[i, h][:, gg, j, :], e_sb[i][:, col : col + 128], ident_bf[:])
+        def e_transpose(i, b, tag):
+            e_flipped[i, b] = psum.tile([P, 2, PACK, P], BF16, tag=tag, bufs=3, name="e_flipped")
+            for g in range(2):
+                for j in range(PACK):
+                    first = BANK * b + CHUNK * g + P * j
+                    nc.tensor.transpose(e_flipped[i, b][:, g, j, :], e_rows[i][:, first : first + P], ident_bf[:])
 
-        def e_exit(i, h, engine, via_gpsimd):
-            if i not in e_grp:
-                e_grp[i] = work.tile([P, T], BF16, tag="e_grp", bufs=2, align_bytes=64, name="e_grp")
-            cols = slice(1024 * h, 1024 * h + 1024)
-            if via_gpsimd:
-                if i not in e_t:
-                    e_t[i] = work.tile([P, T], BF16, tag="e_t", bufs=2, name="e_t")
-                copy_on(engine, e_t[i][:, cols], e_ps[i, h][:].rearrange("p g j n -> p (g j n)"))
+        def e_exit(i, b, engine):
+            if i not in e_grouped:
+                e_grouped[i] = ring.tile([P, T], BF16, tag="e_grouped", align_bytes=64, name="e_grouped")
+            columns = slice(BANK * b, BANK * (b + 1))
+            if i < GPSIMD_TILES:
+                if i not in e_plain:
+                    e_plain[i] = ring.tile([P, T], BF16, tag="e_plain", name="e_plain")
+                copy_on(engine, e_plain[i][:, columns], e_flipped[i, b][:].rearrange("p g j n -> p (g j n)"))
+                nc.gpsimd.tensor_scalar(out=e_grouped[i][:, columns].rearrange("p (g n j) -> p g n j", g=2, j=PACK),
+                                        in0=e_plain[i][:, columns].rearrange("p (g j n) -> p g n j", g=2, j=PACK),
+                                        scalar1=1.0, scalar2=0.0, op0=ALU.mult, op1=ALU.add)
             else:
-                copy_on(engine, e_grp[i][:, cols].rearrange("p (g n j) -> p g n j", g=2, j=4), e_ps[i, h][:].rearrange("p g j n -> p g n j"))
+                copy_on(engine, e_grouped[i][:, columns].rearrange("p (g n j) -> p g n j", g=2, j=PACK),
+                        e_flipped[i, b][:].rearrange("p g j n -> p g n j"))
 
-        def e_regroup(i, h):
-            cols = slice(1024 * h, 1024 * h + 1024)
-            nc.gpsimd.tensor_scalar(out=e_grp[i][:, cols].rearrange("p (g n j) -> p g n j", g=2, j=4),
-                                    in0=e_t[i][:, cols].rearrange("p (g j n) -> p g n j", g=2, j=4),
-                                    scalar1=1.0, scalar2=0.0, op0=ALU.mult, op1=ALU.add)
+        def e_quantise(i, b):
+            if i not in e_codes:
+                e_codes[i] = ring.tile([P, T // PACK], U32, tag="e_codes", bufs=3, align_bytes=64, name="e_codes")
+                e_scales[i] = ring.tile([P, T // PACK], U8, tag="e_scales", bufs=3, align_bytes=64, name="e_scales")
+            words = slice(BANK // PACK * b, BANK // PACK * (b + 1))
+            nc.vector.quantize_mx(out=e_codes[i][:, words].bitcast(FP8X4), scales=e_scales[i][:, words],
+                                  in_=e_grouped[i][:, BANK * b : BANK * (b + 1)])
 
-        def e_quantise(i, h):
-            if i not in e_wd:
-                e_wd[i] = work.tile([P, T // 4], U32, tag="e_wd", bufs=3, align_bytes=64, name="e_wd")
-                e_sc[i] = work.tile([P, T // 4], U8, tag="e_sc", bufs=3, align_bytes=64, name="e_sc")
-            nc.vector.quantize_mx(
-                out=e_wd[i][:, 256 * h : 256 * h + 256].bitcast(FP8X4),
-                scales=e_sc[i][:, 256 * h : 256 * h + 256],
-                in_=e_grp[i][:, 1024 * h : 1024 * h + 1024],
-            )
-
-        def row_scale(i):
-            rinv[i] = work.tile([P, 1], F32, tag="rinv", bufs=4, name="rinv")
-            if rsum[i].shape[1] == 1:
-                nc.vector.reciprocal(out=rinv[i][:], in_=rsum[i][:])
+        def invert_sum(i, pieces):
+            inv_sum[i] = ring.tile([P, 1], F32, tag="inv_sum", bufs=4, name="inv_sum")
+            if pieces == 1:
+                nc.vector.reciprocal(out=inv_sum[i][:], in_=e_sum[i][:])
             else:
-                tot = work.tile([P, 1], F32, tag="tot", name="tot")
-                nc.vector.tensor_reduce(out=tot[:], in_=rsum[i][:], axis=AX.X, op=ALU.add)
-                nc.vector.reciprocal(out=rinv[i][:], in_=tot[:])
+                total = ring.tile([P, 1], F32, tag="total", name="total")
+                nc.vector.tensor_reduce(out=total[:], in_=e_sum[i][:], axis=AX.X, op=ALU.add)
+                nc.vector.reciprocal(out=inv_sum[i][:], in_=total[:])
 
         def value_pass(i, g):
             if g == 0:
-                o_ps[i] = psum.tile([P, VD], F32, tag="o", bufs=2, name="o_ps")
+                o_bank[i] = psum.tile([P, VD], F32, tag="out", bufs=2, name="o_bank")
             nc.tensor.matmul_mx(
-                out=o_ps[i][:],
-                lhsT=e_wd[i][:, P * g : P * g + P].bitcast(FP8X4),
-                lhsT_scale=e_sc[i][:, P * g : P * g + P],
-                rhs=v_words[:, VD * g : VD * g + VD].bitcast(FP8X4),
-                rhs_scale=v_scales[:, VD * g : VD * g + VD],
+                out=o_bank[i][:],
+                lhsT=e_codes[i][:, P * g : P * (g + 1)].bitcast(FP8X4),
+                lhsT_scale=e_scales[i][:, P * g : P * (g + 1)],
+                rhs=v_codes[:, VD * g : VD * (g + 1)].bitcast(FP8X4),
+                rhs_scale=v_scales[:, VD * g : VD * (g + 1)],
                 start=(g == 0),
-                stop=(g == TC - 1),
+                stop=(g == CHUNKS - 1),
             )
 
-        out_view = out.rearrange("(p i) d -> p i d", i=NT)
+        out_view = out.rearrange("(p i) d -> p i d", i=TILES)
 
-        def store(i, engine):
-            o_sb = work.tile([P, VD], F32, tag="o_sb", bufs=3, name="o_sb")
-            if engine == "V":
-                nc.vector.tensor_scalar(out=o_sb[:], in0=o_ps[i][:], scalar1=rinv[i][:], scalar2=None, op0=ALU.mult)
-            else:
-                nc.scalar.activation(out=o_sb[:], in_=o_ps[i][:], func=ACT.Copy, scale=rinv[i][:])
-            nc.sync.dma_start(out=out_view[:, i, :], in_=o_sb[:])
+        def store(i):
+            result = ring.tile([P, VD], F32, tag="result", bufs=3, name="result")
+            nc.vector.tensor_scalar(out=result[:], in0=o_bank[i][:], scalar1=inv_sum[i][:], scalar2=None, op0=ALU.mult)
+            nc.sync.dma_start(out=out_view[:, i, :], in_=result[:])
 
         load()
-        table("Sqrt")
-        sumsq(3, "V")
-        sumsq(1, "S")
-        sumsq(0, "S")
-        sumsq(2, "V")
-        sumsq(4, "S")
-        sumsq(6, "V")
-        sumsq(7, "V")
+        load_table(ACT.Sqrt, 0)
+        for i in (0, 2, 4):
+            sum_squares(i, "S")
+        for i in (1, 3, 5, 7):
+            sum_squares(i, "V")
         norm_sqrt(0)
-        norm_floor(0)
-        norm_recip(0)
-        k_transpose(0, 1)
-        scale(1)
-        v_regroup(4, "G")
+        sum_squares(6, "S")
+        norm_sqrt(1)
+        load_table(ACT.Exp, 1)
+        norm_invert(0)
+        normalise(0)
+        normalise(1)
         k_transpose(0, 0)
-        scale(0)
+        k_transpose(0, 1)
         k_transpose(1, 0)
-        sumsq(5, "S")
         q_transpose(0)
+        for g in GPSIMD_VALUE_CHUNKS:
+            v_regroup(g, "G")
         k_exit(0, 0, "V")
         k_exit(0, 1, "V")
-        norm_sqrt(1)
         k_quantise(0)
         k_transpose(1, 1)
-        scale(3)
         k_transpose(2, 0)
-        norm_floor(1)
+        norm_invert(1)
+        normalise(2)
+        normalise(3)
         k_exit(1, 0, "V")
-        norm_recip(1)
-        scale(2)
-        table("Exp")
         q_exit(0, "S")
-        scale(6)
+        normalise(6)
+        normalise(7)
         q_quantise(0)
         k_exit(1, 1, "S")
-        k_transpose(2, 1)
-        scale(7)
-        k_exit(2, 0, "S")
         k_quantise(1)
-        k_transpose(3, 0)
+        k_transpose(2, 1)
+        k_exit(2, 0, "S")
         k_exit(2, 1, "S")
+        k_transpose(3, 0)
         score_pass(0, 0)
         k_transpose(3, 1)
-        v_regroup(2, "G")
         k_exit(3, 1, "S")
-        v_regroup(5, "G")
-        k_transpose(4, 0)
-        k_transpose(4, 1)
-        scale(5)
-        v_regroup(3, "G")
+        normalise(5)
         k_exit(3, 0, "V")
         k_quantise(2)
+        k_transpose(4, 0)
+        k_transpose(4, 1)
         k_exit(4, 0, "S")
-        score_pass(0, 1)
-        score_exit(0, 0)
-        score_pass(0, 2)
-        k_quantise(3)
-        score_exit(0, 2)
         k_exit(4, 1, "S")
-        k_quantise(4)
+        score_pass(0, 1)
+        score_pass(0, 2)
+        score_exit(0, 0)
+        k_quantise(3)
         score_exit(0, 1)
+        k_quantise(4)
+        score_exit(0, 2)
         k_transpose(5, 0)
         k_transpose(5, 1)
         q_transpose(1)
         k_exit(5, 0, "S")
         k_exit(5, 1, "S")
-        score_pass(0, 4)
-        scale(4)
         q_exit(1, "S")
-        score_pass(0, 3)
+        normalise(4)
         k_quantise(5)
-        score_pass(0, 5)
-        score_exit(0, 3)
-        score_exit(0, 4)
-        score_exit(0, 5)
-        v_regroup(0, "S")
-        bias(0)
+        for c in (3, 4, 5):
+            score_pass(0, c)
+        for c in (3, 4, 5):
+            score_exit(0, c)
+        v_regroup(SCALAR_VALUE_CHUNKS[0], "S")
+        row_bias(0)
         q_quantise(1)
-        exponential(0, 0, 6)
-        v_regroup(1, "S")
-        score_pass(1, 0)
-        score_exit(1, 0)
-        score_pass(1, 1)
-        score_exit(1, 1)
-        score_pass(1, 2)
-        score_exit(1, 2)
-        score_pass(1, 3)
-        score_exit(1, 3)
-        score_pass(1, 4)
-        score_exit(1, 4)
-        score_pass(1, 5)
-        score_exit(1, 5)
-        bias(1)
-        q_transpose(2)
-        q_transpose(3)
-        v_quantise(0)
-        v_quantise(2)
-        q_exit(2, "S")
-        q_exit(3, "S")
-        exponential(1, 0, 6)
-        score_pass(2, 0)
-        score_exit(2, 0)
-        score_pass(2, 1)
-        score_exit(2, 1)
-        score_pass(2, 2)
-        score_exit(2, 2)
-        score_pass(2, 3)
-        score_exit(2, 3)
-        score_pass(2, 4)
-        score_exit(2, 4)
-        score_pass(2, 5)
-        score_exit(2, 5)
-        bias(2)
-        e_transpose(0, 0, "t")
-        e_transpose(0, 1, "t")
-        e_transpose(0, 2, "t")
-        q_quantise(2)
-        q_quantise(3)
-        v_quantise(1)
-        v_quantise(3)
-        e_exit(0, 0, "V", True)
-        e_regroup(0, 0)
-        e_exit(0, 1, "S", True)
-        e_regroup(0, 1)
-        e_exit(0, 2, "S", True)
-        e_regroup(0, 2)
-        exponential(2, 0, 6)
-        score_pass(3, 0)
-        score_exit(3, 0)
-        score_pass(3, 1)
-        score_exit(3, 1)
-        score_pass(3, 2)
-        score_exit(3, 2)
-        score_pass(3, 3)
-        score_exit(3, 3)
-        score_pass(3, 4)
-        score_exit(3, 4)
-        score_pass(3, 5)
-        score_exit(3, 5)
-        bias(3)
-        e_transpose(1, 0, "t")
-        e_transpose(1, 1, "t")
-        e_transpose(1, 2, "t")
-        v_quantise(4)
-        v_quantise(5)
-        e_quantise(0, 0)
-        e_quantise(0, 1)
-        e_quantise(0, 2)
-        row_scale(0)
-        e_exit(1, 0, "S", True)
-        e_regroup(1, 0)
-        e_exit(1, 1, "S", True)
-        e_regroup(1, 1)
-        e_exit(1, 2, "S", True)
-        e_regroup(1, 2)
-        exponential(3, 0, 6)
-        score_pass(4, 0)
-        value_pass(0, 0)
-        score_exit(4, 0)
-        score_pass(4, 1)
-        value_pass(0, 1)
-        score_exit(4, 1)
-        score_pass(4, 2)
-        value_pass(0, 2)
-        score_exit(4, 2)
-        score_pass(4, 3)
-        value_pass(0, 3)
-        score_exit(4, 3)
-        score_pass(4, 4)
-        value_pass(0, 4)
-        score_exit(4, 4)
-        score_pass(4, 5)
-        value_pass(0, 5)
-        score_exit(4, 5)
-        bias(4)
-        e_transpose(2, 0, "t")
-        e_transpose(2, 1, "t")
-        e_transpose(2, 2, "t")
-        e_quantise(1, 0)
-        e_quantise(1, 1)
-        e_quantise(1, 2)
-        row_scale(1)
-        store(0, "S")
-        e_exit(2, 0, "S", True)
-        e_regroup(2, 0)
-        e_exit(2, 1, "S", True)
-        e_regroup(2, 1)
-        e_exit(2, 2, "V", True)
-        e_regroup(2, 2)
-        exponential(4, 0, 6)
-        score_pass(5, 0)
-        value_pass(1, 0)
-        score_exit(5, 0)
-        score_pass(5, 1)
-        value_pass(1, 1)
-        score_exit(5, 1)
-        score_pass(5, 2)
-        value_pass(1, 2)
-        score_exit(5, 2)
-        score_pass(5, 3)
-        value_pass(1, 3)
-        score_exit(5, 3)
-        score_pass(5, 4)
-        value_pass(1, 4)
-        score_exit(5, 4)
-        score_pass(5, 5)
-        value_pass(1, 5)
-        score_exit(5, 5)
-        bias(5)
-        e_transpose(3, 0, "t")
-        e_transpose(3, 1, "t")
-        e_transpose(3, 2, "t")
-        e_quantise(2, 0)
-        e_quantise(2, 1)
-        e_quantise(2, 2)
-        row_scale(2)
-        store(1, "V")
-        e_exit(3, 0, "S", True)
-        e_regroup(3, 0)
-        e_exit(3, 1, "S", True)
-        e_regroup(3, 1)
-        e_exit(3, 2, "S", True)
-        e_regroup(3, 2)
-        exponential(5, 0, 6)
-        score_pass(6, 0)
-        value_pass(2, 0)
-        score_exit(6, 0)
-        score_pass(6, 1)
-        value_pass(2, 1)
-        score_exit(6, 1)
-        score_pass(6, 2)
-        value_pass(2, 2)
-        score_exit(6, 2)
-        score_pass(6, 3)
-        value_pass(2, 3)
-        score_exit(6, 3)
-        score_pass(6, 4)
-        value_pass(2, 4)
-        score_exit(6, 4)
-        score_pass(6, 5)
-        value_pass(2, 5)
-        score_exit(6, 5)
-        bias(6)
-        e_transpose(4, 0, "t")
-        e_transpose(4, 1, "t")
-        e_transpose(4, 2, "t")
-        e_quantise(3, 0)
-        e_quantise(3, 1)
-        e_quantise(3, 2)
-        row_scale(3)
-        store(2, "V")
-        e_exit(4, 0, "S", True)
-        e_regroup(4, 0)
-        e_exit(4, 1, "S", True)
-        e_regroup(4, 1)
-        e_exit(4, 2, "S", True)
-        e_regroup(4, 2)
-        exponential(6, 0, 6)
-        score_pass(7, 0)
-        value_pass(3, 0)
-        score_exit(7, 0)
-        score_pass(7, 1)
-        value_pass(3, 1)
-        score_exit(7, 1)
-        score_pass(7, 2)
-        value_pass(3, 2)
-        score_exit(7, 2)
-        score_pass(7, 3)
-        value_pass(3, 3)
-        score_exit(7, 3)
-        score_pass(7, 4)
-        value_pass(3, 4)
-        score_exit(7, 4)
-        score_pass(7, 5)
-        value_pass(3, 5)
-        score_exit(7, 5)
-        bias(7)
-        e_transpose(5, 0, "t")
-        e_transpose(5, 1, "t")
-        e_transpose(5, 2, "t")
-        e_quantise(4, 0)
-        e_quantise(4, 1)
-        e_quantise(4, 2)
-        row_scale(4)
-        store(3, "V")
-        e_exit(5, 0, "V", True)
-        value_pass(4, 0)
-        e_exit(5, 1, "S", True)
-        e_regroup(5, 1)
-        e_regroup(5, 0)
-        e_exit(5, 2, "V", True)
-        e_regroup(5, 2)
-        value_pass(4, 1)
-        value_pass(4, 2)
-        exponential(7, 2, 4)
-        exponential(7, 0, 2)
-        value_pass(4, 3)
-        value_pass(4, 4)
-        value_pass(4, 5)
-        e_transpose(6, 0, "t")
-        exponential(7, 4, 6)
-        store(4, "V")
-        e_transpose(6, 1, "t")
-        e_transpose(7, 1, "s")
-        e_transpose(6, 2, "t")
-        e_exit(6, 0, "V", False)
-        e_exit(6, 1, "V", False)
-        e_quantise(5, 0)
-        e_transpose(7, 0, "s")
-        e_quantise(5, 2)
-        e_transpose(7, 2, "s")
-        e_quantise(5, 1)
-        value_pass(5, 0)
-        value_pass(5, 1)
-        value_pass(5, 2)
-        e_exit(6, 2, "S", False)
-        e_quantise(6, 0)
-        value_pass(5, 3)
-        row_scale(5)
-        e_quantise(6, 1)
-        e_quantise(6, 2)
-        value_pass(5, 4)
-        e_exit(7, 0, "S", False)
-        e_exit(7, 2, "V", False)
-        value_pass(5, 5)
-        value_pass(6, 0)
-        value_pass(6, 1)
-        e_exit(7, 1, "S", False)
-        store(5, "V")
-        value_pass(6, 2)
-        value_pass(6, 3)
-        e_quantise(7, 0)
-        value_pass(6, 4)
-        value_pass(6, 5)
-        value_pass(7, 0)
-        value_pass(7, 1)
-        row_scale(7)
-        e_quantise(7, 1)
-        value_pass(7, 2)
-        value_pass(7, 3)
-        row_scale(6)
-        e_quantise(7, 2)
-        value_pass(7, 4)
-        value_pass(7, 5)
-        store(6, "V")
-        store(7, "V")
+
+        for p in range(TILES - 1):
+            if p == 1:
+                q_exit(2, "S")
+                q_exit(3, "S")
+            if p >= 2:
+                for b in range(BANKS):
+                    e_exit(p - 2, b, "S")
+            exponential(p, 0, 1)
+            if p == 0:
+                v_regroup(SCALAR_VALUE_CHUNKS[1], "S")
+            for c in range(CHUNKS):
+                score_pass(p + 1, c)
+                if p >= 3:
+                    value_pass(p - 3, c)
+                score_exit(p + 1, c)
+            row_bias(p + 1)
+            if p >= 1:
+                for b in range(BANKS):
+                    e_transpose(p - 1, b, "flip")
+            if p == 0:
+                q_transpose(2)
+                q_transpose(3)
+            if p == 1:
+                q_quantise(2)
+                q_quantise(3)
+            if p < len(VALUE_QUANTISE_ORDER):
+                for g in VALUE_QUANTISE_ORDER[p]:
+                    v_quantise(g)
+            if p >= 2:
+                for b in range(BANKS):
+                    e_quantise(p - 2, b)
+                invert_sum(p - 2, 1)
+            if p >= 3:
+                store(p - 3)
+
+        last = TILES - 1
+        e_exit(last - 2, 0, "V")
+        e_exit(last - 2, 1, "S")
+        e_exit(last - 2, 2, "V")
+        for g in range(CHUNKS):
+            value_pass(last - 3, g)
+        for piece in range(BANKS):
+            exponential(last, piece, BANKS)
+        for b in range(BANKS):
+            e_transpose(last - 1, b, "flip")
+        for b in range(BANKS):
+            e_transpose(last, b, "score")
+        store(last - 3)
+        e_exit(last - 1, 0, "V")
+        e_exit(last - 1, 1, "V")
+        e_exit(last - 1, 2, "S")
+        for i in (last - 2, last - 1):
+            for b in range(BANKS):
+                e_quantise(i, b)
+            invert_sum(i, 1)
+            for g in range(CHUNKS):
+                value_pass(i, g)
+        e_exit(last, 0, "S")
+        e_exit(last, 1, "S")
+        e_exit(last, 2, "V")
+        store(last - 2)
+        for b in range(BANKS):
+            e_quantise(last, b)
+        invert_sum(last, BANKS)
+        for g in range(CHUNKS):
+            value_pass(last, g)
+        store(last - 1)
+        store(last)

@@ -26,8 +26,8 @@ FLOPS = 2 * N * T * QK + 2 * N * T * VD
 
 GPSIMD_TILES = TILES - 2
 SCALAR_VALUE_CHUNKS = (0, 1)
-GPSIMD_VALUE_CHUNKS = (5, 2, 3, 4)
-VALUE_QUANTISE_ORDER = ((0, 5), (1, 2), (3, 4))
+GPSIMD_VALUE_CHUNKS = (4, 2, 5, 3)
+VALUE_QUANTISE_ORDER = ((0, 2), (1, 3), (4, 5))
 
 
 def tile_contextrcnn_pb_kernel(tc, q_emb, keys, values, out):
@@ -44,15 +44,17 @@ def tile_contextrcnn_pb_kernel(tc, q_emb, keys, values, out):
             else:
                 nc.scalar.copy(out=out_ap, in_=in_ap)
 
+        def half(h):
+            return slice(TILES // 2 * h, TILES // 2 * (h + 1))
+
         q_raw = keep.tile([P, TILES, QK], BF16, name="q_raw")
         k_raw = []
         v_raw = []
 
         def load():
             q_view = q_emb.rearrange("(p i) k -> p i k", i=TILES)
-            for pair in range(TILES // 2):
-                tiles = slice(2 * pair, 2 * pair + 2)
-                nc.sync.dma_start(out=q_raw[:, tiles, :], in_=q_view[:, tiles, :])
+            for h in range(2):
+                nc.sync.dma_start(out=q_raw[:, half(h), :], in_=q_view[:, half(h), :])
             for c in range(CHUNKS):
                 rows = keep.tile([P, PACK, QK], BF16, name="k_raw%d" % c)
                 nc.sync.dma_start(out=rows[:], in_=keys[CHUNK * c : CHUNK * (c + 1), :].rearrange("(p a) k -> p a k", a=PACK))
@@ -90,9 +92,6 @@ def tile_contextrcnn_pb_kernel(tc, q_emb, keys, values, out):
                 squares = ring.tile([P, QK], F32, tag="squares_f", name="squares_f")
                 nc.vector.scalar_tensor_tensor(out=squares[:], in0=q_raw[:, i, :], scalar=1.0, in1=q_raw[:, i, :],
                                                op0=ALU.mult, op1=ALU.mult, accum_out=sumsq[:, i, 0:1])
-
-        def half(h):
-            return slice(TILES // 2 * h, TILES // 2 * (h + 1))
 
         def norm_sqrt(h):
             nc.scalar.activation(out=norm[:, half(h)], in_=sumsq[:, half(h), 0], func=ACT.Sqrt)
@@ -258,12 +257,12 @@ def tile_contextrcnn_pb_kernel(tc, q_emb, keys, values, out):
 
         load()
         load_table(ACT.Sqrt, 0)
-        for i in (0, 2, 4):
+        for i in (0, 1, 4):
             sum_squares(i, "S")
-        for i in (1, 3, 5, 7):
+        for i in (2, 3, 6, 7):
             sum_squares(i, "V")
         norm_sqrt(0)
-        sum_squares(6, "S")
+        sum_squares(5, "S")
         norm_sqrt(1)
         load_table(ACT.Exp, 1)
         norm_invert(0)

from contextlib import ExitStack

import concourse.mybir as mybir
from concourse.masks import make_identity

F32 = mybir.dt.float32
BF16 = mybir.dt.bfloat16
U32 = mybir.dt.uint32
U8 = mybir.dt.uint8
FP8X4 = mybir.dt.float8_e4m3fn_x4
ALU = mybir.AluOpType
ACT = mybir.ActivationFunctionType
AX = mybir.AxisListType

P = 128
PACK = 4
N, T, QK, VD = 1024, 3072, 512, 512
CHUNK = P * PACK
TILES = N // P
CHUNKS = T // CHUNK
BANK = 2 * CHUNK
BANKS = T // BANK
SOFTMAX_SCALE = 6.25
NORM_FLOOR = 1e-12
FLOPS = 2 * N * T * QK + 2 * N * T * VD

GPSIMD_TILES = TILES - 2
SCALAR_VALUE_CHUNKS = (0, 1)
GPSIMD_VALUE_CHUNKS = (4, 2, 5, 3)
VALUE_QUANTISE_ORDER = ((0, 2), (1, 3), (4, 5))


def tile_contextrcnn_pb_kernel(tc, q_emb, keys, values, out):
    nc = tc.nc
    with ExitStack() as ctx:
        ctx.enter_context(tc.manual_schedule())
        keep = ctx.enter_context(tc.tile_pool(name="keep", bufs=1))
        ring = ctx.enter_context(tc.tile_pool(name="ring", bufs=2))
        psum = ctx.enter_context(tc.psum_pool(name="psum", bufs=1))

        def copy_on(engine, out_ap, in_ap):
            if engine == "V":
                nc.vector.tensor_copy(out=out_ap, in_=in_ap)
            else:
                nc.scalar.copy(out=out_ap, in_=in_ap)

        def half(h):
            return slice(TILES // 2 * h, TILES // 2 * (h + 1))

        q_raw = keep.tile([P, TILES, QK], BF16, name="q_raw")
        k_raw = []
        v_raw = []

        def load():
            q_view = q_emb.rearrange("(p i) k -> p i k", i=TILES)
            for h in range(2):
                nc.sync.dma_start(out=q_raw[:, half(h), :], in_=q_view[:, half(h), :])
            for c in range(CHUNKS):
                rows = keep.tile([P, PACK, QK], BF16, name="k_raw%d" % c)
                nc.sync.dma_start(out=rows[:], in_=keys[CHUNK * c : CHUNK * (c + 1), :].rearrange("(p a) k -> p a k", a=PACK))
                k_raw.append(rows)
            for g in range(CHUNKS):
                rows = keep.tile([P, PACK, VD], BF16, name="v_raw%d" % g)
                nc.sync.dma_start(out=rows[:], in_=values[CHUNK * g : CHUNK * (g + 1), :].rearrange("(p j) w -> p j w", j=PACK))
                v_raw.append(rows)

        ident_bf = keep.tile([P, P], BF16, name="ident_bf")
        make_identity(nc, ident_bf[:])
        ident_f = keep.tile([P, P], F32, name="ident_f")
        make_identity(nc, ident_f[:])
        one = keep.tile([P, 1], F32, name="one")
        nc.vector.memset(one[:], 1.0)
        warm = keep.tile([P, 2], F32, name="warm")

        def load_table(func, column):
            nc.scalar.activation(out=warm[:, column : column + 1], in_=one[:], func=func)

        sumsq = keep.tile([P, TILES, 8], F32, name="sumsq")
        norm = keep.tile([P, TILES], F32, name="norm")
        norm_floored = keep.tile([P, TILES], F32, name="norm_floored")
        inv_norm = keep.tile([P, TILES], F32, name="inv_norm")
        q_hat = keep.tile([P, TILES, QK], BF16, name="q_hat")
        q_codes = keep.tile([P, N], U32, name="q_codes", align_bytes=64)
        q_scales = keep.tile([P, N], U8, name="q_scales", align_bytes=64)
        q_flipped, q_grouped = {}, {}

        def sum_squares(i, engine):
            if engine == "S":
                squares = ring.tile([P, QK], BF16, tag="squares_bf", name="squares_bf")
                nc.scalar.activation(out=squares[:], in_=q_raw[:, i, :], func=ACT.Square, accum_out=sumsq[:, i, 0:1])
            else:
                squares = ring.tile([P, QK], F32, tag="squares_f", name="squares_f")
                nc.vector.scalar_tensor_tensor(out=squares[:], in0=q_raw[:, i, :], scalar=1.0, in1=q_raw[:, i, :],
                                               op0=ALU.mult, op1=ALU.mult, accum_out=sumsq[:, i, 0:1])

        def norm_sqrt(h):
            nc.scalar.activation(out=norm[:, half(h)], in_=sumsq[:, half(h), 0], func=ACT.Sqrt)

        def norm_invert(h):
            nc.vector.tensor_scalar_max(out=norm_floored[:, half(h)], in0=norm[:, half(h)], scalar1=NORM_FLOOR)
            nc.vector.reciprocal(out=inv_norm[:, half(h)], in_=norm_floored[:, half(h)])

        def normalise(i):
            nc.vector.tensor_scalar(out=q_hat[:, i, :], in0=q_raw[:, i, :], scalar1=inv_norm[:, i : i + 1], scalar2=None, op0=ALU.mult)

        def q_transpose(pair):
            q_flipped[pair] = psum.tile([P, 2, PACK, P], BF16, tag="out", bufs=2, name="q_flipped")
            for i in range(2):
                columns = q_hat[:, 2 * pair + i, :].rearrange("p (u m e) -> p u e m", u=2, e=2)
                for u in range(2):
                    for e in range(2):
                        nc.tensor.transpose(q_flipped[pair][:, i, 2 * u + e, :], columns[:, u, e, :], ident_bf[:])

        def q_exit(pair, engine):
            q_grouped[pair] = ring.tile([P, 2 * P * PACK], BF16, tag="q_grouped", align_bytes=64, name="q_grouped")
            copy_on(engine, q_grouped[pair][:].rearrange("p (i n t) -> p i n t", i=2, t=PACK),
                    q_flipped[pair][:].rearrange("p i t n -> p i n t"))

        def q_quantise(pair):
            columns = slice(2 * P * pair, 2 * P * (pair + 1))
            nc.vector.quantize_mx(out=q_codes[:, columns].bitcast(FP8X4), scales=q_scales[:, columns], in_=q_grouped[pair][:])

        k_codes = keep.tile([P, T], U32, name="k_codes", align_bytes=64)
        k_scales = keep.tile([P, T], U8, name="k_scales", align_bytes=64)
        k_flipped, k_grouped = {}, {}

        def k_transpose(c, h):
            words = k_raw[c][:].rearrange("p a k -> p (a k)").bitcast(F32)
            k_flipped[c, h] = psum.tile([P, 2, 2, P], F32, tag="flip", bufs=3, name="k_flipped")
            for a in range(2):
                for u in range(2):
                    first = QK // 2 * (2 * h + a) + P * u
                    nc.tensor.transpose(k_flipped[c, h][:, a, u, :], words[:, first : first + P], ident_f[:])

        def k_exit(c, h, engine):
            if c not in k_grouped:
                k_grouped[c] = ring.tile([P, CHUNK * PACK], BF16, tag="k_grouped", align_bytes=64, name="k_grouped")
            words = k_grouped[c][:].bitcast(F32).rearrange("p (a t u) -> p a t u", a=PACK, u=2)
            copy_on(engine, words[:, 2 * h : 2 * h + 2, :, :], k_flipped[c, h][:].rearrange("p a u t -> p a t u"))

        def k_quantise(c):
            columns = slice(CHUNK * c, CHUNK * (c + 1))
            nc.vector.quantize_mx(out=k_codes[:, columns].bitcast(FP8X4), scales=k_scales[:, columns], in_=k_grouped[c][:])

        v_codes = keep.tile([P, CHUNKS * VD], U32, name="v_codes", align_bytes=64)
        v_scales = keep.tile([P, CHUNKS * VD], U8, name="v_scales", align_bytes=64)
        v_grouped = {}

        def v_regroup(g, engine):
            v_grouped[g] = ring.tile([P, VD, PACK], BF16, tag="v_grouped", bufs=CHUNKS, align_bytes=64, name="v_grouped")
            if engine == "G":
                for part in range(2):
                    w = slice(VD // 2 * part, VD // 2 * (part + 1))
                    nc.gpsimd.tensor_scalar(out=v_grouped[g][:, w, :], in0=v_raw[g][:, :, w].rearrange("p j w -> p w j"),
                                            scalar1=1.0, scalar2=0.0, op0=ALU.mult, op1=ALU.add)
            else:
                copy_on(engine, v_grouped[g][:].rearrange("p (c i) j -> p c j i", i=4), v_raw[g][:].rearrange("p j (c i) -> p c j i", i=4))

        def v_quantise(g):
            columns = slice(VD * g, VD * (g + 1))
            nc.vector.quantize_mx(out=v_codes[:, columns].bitcast(FP8X4), scales=v_scales[:, columns],
                                  in_=v_grouped[g][:].rearrange("p w j -> p (w j)"))

        s_bank, s_neg, bank_min, exp_bias = {}, {}, {}, {}
        e_rows, e_sum, e_flipped, e_plain, e_grouped, e_codes, e_scales = {}, {}, {}, {}, {}, {}, {}
        inv_sum, o_bank = {}, {}

        def score_pass(i, c):
            s_bank[i, c] = psum.tile([P, CHUNK], F32, tag="score", bufs=3, name="s_bank")
            nc.tensor.matmul_mx(
                out=s_bank[i, c][:],
                lhsT=q_codes[:, P * i : P * (i + 1)].bitcast(FP8X4),
                lhsT_scale=q_scales[:, P * i : P * (i + 1)],
                rhs=k_codes[:, CHUNK * c : CHUNK * (c + 1)].bitcast(FP8X4),
                rhs_scale=k_scales[:, CHUNK * c : CHUNK * (c + 1)],
                start=True,
                stop=True,
            )

        def score_exit(i, c):
            if i not in s_neg:
                s_neg[i] = ring.tile([P, T], F32, tag="s_neg", name="s_neg")
                bank_min[i] = ring.tile([P, CHUNKS], F32, tag="bank_min", bufs=3, name="bank_min")
            nc.vector.tensor_scalar(out=s_neg[i][:, CHUNK * c : CHUNK * (c + 1)], in0=s_bank[i, c][:], scalar1=-SOFTMAX_SCALE, scalar2=None,
                                    op0=ALU.mult, op1=ALU.min, accum_out=bank_min[i][:, c : c + 1])

        def row_bias(i):
            exp_bias[i] = ring.tile([P, 1], F32, tag="exp_bias", bufs=3, name="exp_bias")
            nc.vector.tensor_reduce(out=exp_bias[i][:], in_=bank_min[i][:], axis=AX.X, op=ALU.min)

        def exponential(i, piece, pieces):
            if i not in e_rows:
                e_rows[i] = ring.tile([P, T], BF16, tag="e_rows", name="e_rows")
                e_sum[i] = ring.tile([P, pieces], F32, tag="e_sum", bufs=5, name="e_sum")
            columns = slice(T // pieces * piece, T // pieces * (piece + 1))
            nc.scalar.activation(out=e_rows[i][:, columns], in_=s_neg[i][:, columns], func=ACT.Exp, bias=exp_bias[i][:], scale=-1.0,
                                 accum_out=e_sum[i][:, piece : piece + 1])

        def e_transpose(i, b, tag):
            e_flipped[i, b] = psum.tile([P, 2, PACK, P], BF16, tag=tag, bufs=3, name="e_flipped")
            for g in range(2):
                for j in range(PACK):
                    first = BANK * b + CHUNK * g + P * j
                    nc.tensor.transpose(e_flipped[i, b][:, g, j, :], e_rows[i][:, first : first + P], ident_bf[:])

        def e_exit(i, b, engine):
            if i not in e_grouped:
                e_grouped[i] = ring.tile([P, T], BF16, tag="e_grouped", align_bytes=64, name="e_grouped")
            columns = slice(BANK * b, BANK * (b + 1))
            if i < GPSIMD_TILES:
                if i not in e_plain:
                    e_plain[i] = ring.tile([P, T], BF16, tag="e_plain", name="e_plain")
                copy_on(engine, e_plain[i][:, columns], e_flipped[i, b][:].rearrange("p g j n -> p (g j n)"))
                nc.gpsimd.tensor_scalar(out=e_grouped[i][:, columns].rearrange("p (g n j) -> p g n j", g=2, j=PACK),
                                        in0=e_plain[i][:, columns].rearrange("p (g j n) -> p g n j", g=2, j=PACK),
                                        scalar1=1.0, scalar2=0.0, op0=ALU.mult, op1=ALU.add)
            else:
                copy_on(engine, e_grouped[i][:, columns].rearrange("p (g n j) -> p g n j", g=2, j=PACK),
                        e_flipped[i, b][:].rearrange("p g j n -> p g n j"))

        def e_quantise(i, b):
            if i not in e_codes:
                e_codes[i] = ring.tile([P, T // PACK], U32, tag="e_codes", bufs=3, align_bytes=64, name="e_codes")
                e_scales[i] = ring.tile([P, T // PACK], U8, tag="e_scales", bufs=3, align_bytes=64, name="e_scales")
            words = slice(BANK // PACK * b, BANK // PACK * (b + 1))
            nc.vector.quantize_mx(out=e_codes[i][:, words].bitcast(FP8X4), scales=e_scales[i][:, words],
                                  in_=e_grouped[i][:, BANK * b : BANK * (b + 1)])

        def invert_sum(i, pieces):
            inv_sum[i] = ring.tile([P, 1], F32, tag="inv_sum", bufs=4, name="inv_sum")
            if pieces == 1:
                nc.vector.reciprocal(out=inv_sum[i][:], in_=e_sum[i][:])
            else:
                total = ring.tile([P, 1], F32, tag="total", name="total")
                nc.vector.tensor_reduce(out=total[:], in_=e_sum[i][:], axis=AX.X, op=ALU.add)
                nc.vector.reciprocal(out=inv_sum[i][:], in_=total[:])

        def value_pass(i, g):
            if g == 0:
                o_bank[i] = psum.tile([P, VD], F32, tag="out", bufs=2, name="o_bank")
            nc.tensor.matmul_mx(
                out=o_bank[i][:],
                lhsT=e_codes[i][:, P * g : P * (g + 1)].bitcast(FP8X4),
                lhsT_scale=e_scales[i][:, P * g : P * (g + 1)],
                rhs=v_codes[:, VD * g : VD * (g + 1)].bitcast(FP8X4),
                rhs_scale=v_scales[:, VD * g : VD * (g + 1)],
                start=(g == 0),
                stop=(g == CHUNKS - 1),
            )

        out_view = out.rearrange("(p i) d -> p i d", i=TILES)

        def store(i):
            result = ring.tile([P, VD], F32, tag="result", bufs=3, name="result")
            nc.vector.tensor_scalar(out=result[:], in0=o_bank[i][:], scalar1=inv_sum[i][:], scalar2=None, op0=ALU.mult)
            nc.sync.dma_start(out=out_view[:, i, :], in_=result[:])

        load()
        load_table(ACT.Sqrt, 0)
        for i in (0, 1, 4):
            sum_squares(i, "S")
        for i in (2, 3, 6, 7):
            sum_squares(i, "V")
        norm_sqrt(0)
        sum_squares(5, "S")
        norm_sqrt(1)
        load_table(ACT.Exp, 1)
        norm_invert(0)
        normalise(0)
        normalise(1)
        k_transpose(0, 0)
        k_transpose(0, 1)
        k_transpose(1, 0)
        q_transpose(0)
        for g in GPSIMD_VALUE_CHUNKS:
            v_regroup(g, "G")
        k_exit(0, 0, "V")
        k_exit(0, 1, "V")
        k_quantise(0)
        k_transpose(1, 1)
        k_transpose(2, 0)
        norm_invert(1)
        normalise(2)
        normalise(3)
        k_exit(1, 0, "V")
        q_exit(0, "S")
        normalise(6)
        normalise(7)
        q_quantise(0)
        k_exit(1, 1, "S")
        k_quantise(1)
        k_transpose(2, 1)
        k_exit(2, 0, "S")
        k_exit(2, 1, "S")
        k_transpose(3, 0)
        score_pass(0, 0)
        k_transpose(3, 1)
        k_exit(3, 1, "S")
        normalise(5)
        k_exit(3, 0, "V")
        k_quantise(2)
        k_transpose(4, 0)
        k_transpose(4, 1)
        k_exit(4, 0, "S")
        k_exit(4, 1, "S")
        score_pass(0, 1)
        score_pass(0, 2)
        score_exit(0, 0)
        k_quantise(3)
        score_exit(0, 1)
        k_quantise(4)
        score_exit(0, 2)
        k_transpose(5, 0)
        k_transpose(5, 1)
        q_transpose(1)
        k_exit(5, 0, "S")
        k_exit(5, 1, "S")
        q_exit(1, "S")
        normalise(4)
        k_quantise(5)
        for c in (3, 4, 5):
            score_pass(0, c)
        for c in (3, 4, 5):
            score_exit(0, c)
        v_regroup(SCALAR_VALUE_CHUNKS[0], "S")
        row_bias(0)
        q_quantise(1)

        for p in range(TILES - 1):
            if p == 1:
                q_exit(2, "S")
                q_exit(3, "S")
            if p >= 2:
                for b in range(BANKS):
                    e_exit(p - 2, b, "S")
            exponential(p, 0, 1)
            if p == 0:
                v_regroup(SCALAR_VALUE_CHUNKS[1], "S")
            for c in range(CHUNKS):
                score_pass(p + 1, c)
                if p >= 3:
                    value_pass(p - 3, c)
                score_exit(p + 1, c)
            row_bias(p + 1)
            if p >= 1:
                for b in range(BANKS):
                    e_transpose(p - 1, b, "flip")
            if p == 0:
                q_transpose(2)
                q_transpose(3)
            if p == 1:
                q_quantise(2)
                q_quantise(3)
            if p < len(VALUE_QUANTISE_ORDER):
                for g in VALUE_QUANTISE_ORDER[p]:
                    v_quantise(g)
            if p >= 2:
                for b in range(BANKS):
                    e_quantise(p - 2, b)
                invert_sum(p - 2, 1)
            if p >= 3:
                store(p - 3)

        last = TILES - 1
        e_exit(last - 2, 0, "V")
        e_exit(last - 2, 1, "S")
        e_exit(last - 2, 2, "V")
        for g in range(CHUNKS):
            value_pass(last - 3, g)
        for piece in range(BANKS):
            exponential(last, piece, BANKS)
        for b in range(BANKS):
            e_transpose(last - 1, b, "flip")
        for b in range(BANKS):
            e_transpose(last, b, "score")
        store(last - 3)
        e_exit(last - 1, 0, "V")
        e_exit(last - 1, 1, "V")
        e_exit(last - 1, 2, "S")
        for i in (last - 2, last - 1):
            for b in range(BANKS):
                e_quantise(i, b)
            invert_sum(i, 1)
            for g in range(CHUNKS):
                value_pass(i, g)
        e_exit(last, 0, "S")
        e_exit(last, 1, "S")
        e_exit(last, 2, "V")
        store(last - 2)
        for b in range(BANKS):
            e_quantise(last, b)
        invert_sum(last, BANKS)
        for g in range(CHUNKS):
            value_pass(last, g)
        store(last - 1)
        store(last)
